import numpy as np
import ml_dtypes


def mxq(x, axis, fmt="e4m3"):
    dtype, down = {"e4m3": (ml_dtypes.float8_e4m3fn, 7), "e5m2": (ml_dtypes.float8_e5m2, 14)}[fmt]
    v = np.moveaxis(np.asarray(x, np.float32).astype(ml_dtypes.bfloat16).astype(np.float64), axis, -1)
    blocks = v.reshape(v.shape[:-1] + (-1, 32))
    amax = np.abs(blocks).max(-1, keepdims=True)
    byte = np.maximum(np.where(amax > 0, np.frexp(amax)[1] - 1 + 127, 0) - down, 1)
    scale = np.exp2(byte - 127.0)
    codes = (blocks / scale).astype(np.float32).astype(dtype).astype(np.float64)
    return np.moveaxis((codes * scale).reshape(v.shape), -1, axis)


WIDE = False


def mx_kscale(k):
    if not WIDE:
        return np.ones(k)
    levels = np.array([10, -10, 5, -5, 0])
    if k % 512:
        return np.exp2(np.random.permutation(np.resize(levels, k // 32))).repeat(32)
    a = np.empty((k // 512, 16))
    for p in range(k // 512):
        a[p, :8] = np.random.permutation(np.resize(levels, 8))
        for g in range(8):
            far = levels[np.abs(levels - a[p, g]) >= 10]
            a[p, g + 8] = far[np.random.randint(len(far))]
    return np.exp2(a.ravel()).repeat(32)


BF16 = ml_dtypes.bfloat16


def bf(x):
    return np.asarray(x, np.float32).astype(BF16)


def f64(x):
    return np.asarray(x).astype(np.float64)


B, T, C, F = 4, 512, 512, 2048
M = T


def silu(v):
    return v / (1.0 + np.exp(-v))


def sigmoid(v):
    return 1.0 / (1.0 + np.exp(-v))


def setup_inputs():
    t = mx_kscale(F)
    x = np.random.standard_normal((B, T, C)) + 0.5 * np.random.standard_normal((B, 1, C))
    return {"h": bf(silu(np.random.standard_normal((B, T, F)) * 0.85) * t),
            "x": bf(x),
            "memory": bf(np.random.standard_normal((1, M, C)) * 6.0 / np.sqrt(C)),
            "w2": bf(np.random.standard_normal((F, C)) * 3.0 / np.sqrt(F) / t[:, None]),
            "b2": bf(np.random.standard_normal(C) * 0.5)}


def reference(h, x, memory, w2, b2):
    update_gate = sigmoid((mxq(f64(h), 2, "e4m3") @ mxq(f64(w2), 0, "e4m3")) + f64(b2))
    x_mean = f64(x).mean(axis=1, keepdims=True)
    new_mem = f64(memory) * (1.0 - update_gate) + x_mean * update_gate
    return new_mem.mean(axis=0, keepdims=True)

@@ -1,0 +1,322 @@
+from contextlib import ExitStack
+
+import concourse.bass as bass
+import concourse.mybir as mybir
+import concourse.tile as tile
+from concourse.masks import make_identity
+
+F32 = mybir.dt.float32
+BF16 = mybir.dt.bfloat16
+U32 = mybir.dt.uint32
+U8 = mybir.dt.uint8
+FP8X4 = mybir.dt.float8_e4m3fn_x4
+ALU = mybir.AluOpType
+ACT = mybir.ActivationFunctionType
+
+P = 128
+B = 4
+T = 512
+C = 512
+F = 2048
+FLOPS = 2 * B * T * F * C
+
+W_GROUPS_ON_VECTOR = 84
+
+
+def tile_dynamicmemorybank_pb_kernel(tc, h, x, memory, w2, b2, out):
+    nc = tc.nc
+    with ExitStack() as ctx:
+        const = ctx.enter_context(tc.tile_pool(name="const", bufs=1))
+        keep = ctx.enter_context(tc.tile_pool(name="keep", bufs=1))
+        work = ctx.enter_context(tc.tile_pool(name="work", bufs=2))
+        ps_acc = ctx.enter_context(tc.psum_pool(name="psacc", bufs=4))
+        ps_tp = ctx.enter_context(tc.psum_pool(name="pstp", bufs=4))
+        ctx.enter_context(tc.manual_schedule())
+
+        ident32 = const.tile([P, P], F32, name="ident32")
+        identb = const.tile([P, P], BF16, name="identb")
+        ones = const.tile([P, 32], BF16, name="ones")
+        b2rows = const.tile([P, P], BF16, name="b2rows")
+        b2col = const.tile([P, 4], F32, name="b2col")
+        warm = const.tile([P, 2], F32, name="warm")
+        make_identity(nc, ident32[:])
+        make_identity(nc, identb[:])
+        nc.vector.memset(b2rows[:], 0.0)
+        nc.vector.memset(ones[:], 1.0)
+        nc.vector.memset(warm[:], 0.0)
+        nc.scalar.dma_start(out=b2rows[0:4, :], in_=b2.rearrange("(r c) -> r c", r=4))
+        nc.scalar.activation(out=warm[:, 1:2], in_=warm[:, 0:1], func=ACT.Sigmoid)
+
+        w_raw = [keep.tile([P, 4 * C], BF16, name="w_raw%d" % g) for g in range(4)]
+        pieces = {}
+        x_sb = [keep.tile([P, 4 * C], BF16, name="x_sb%d" % b) for b in range(B)]
+        mem_sb = keep.tile([P, 4 * C], BF16, name="mem_sb")
+
+        def load_w(g):
+            nc.sync.dma_start(
+                out=w_raw[g][:],
+                in_=w2[512 * g : 512 * (g + 1), :].rearrange("(p j) c -> p (j c)", j=4),
+            )
+
+        def load_h(b, k0, klen):
+            t = keep.tile([P, 4 * klen], BF16, name="h_%d_%d" % (b, k0))
+            nc.sync.dma_start(
+                out=t[:].rearrange("p (t k) -> p t k", t=4),
+                in_=h[b].rearrange("(p t) k -> p t k", t=4)[:, :, k0 : k0 + klen],
+            )
+            for g in range(k0 // 512, (k0 + klen) // 512):
+                pieces[4 * b + g] = (t, klen, k0)
+
+        def load_x(b):
+            nc.sync.dma_start(out=x_sb[b][:], in_=x[b].rearrange("(p j) c -> p (j c)", j=4))
+
+        for g in range(4):
+            load_w(g)
+            load_h(0, 512 * g, 512)
+        load_h(1, 0, 1024)
+        nc.sync.dma_start(out=mem_sb[:], in_=memory[0].rearrange("(p t) c -> p (t c)", t=4))
+        load_x(0)
+        load_h(1, 1024, 1024)
+        load_h(2, 0, 1024)
+        load_x(1)
+        load_h(2, 1024, 1024)
+        load_h(3, 0, 1024)
+        load_x(2)
+        load_h(3, 1024, 1024)
+        load_x(3)
+
+        wq = keep.tile([P, 4 * C], U32, name="wq", align_bytes=64)
+        ws = keep.tile([P, 4 * C], U8, name="ws", align_bytes=64)
+        memq = keep.tile([P, 4 * T], BF16, name="memq")
+        acc_out = [keep.tile([P, T], F32, name="acc_out%d" % ct) for ct in range(4)]
+        xm4 = [keep.tile([P, 4], F32, name="xm4_%d" % b) for b in range(B)]
+
+        state = {}
+
+        def copy_on(eng, out_ap, in_ap):
+            if eng == "V":
+                nc.vector.tensor_copy(out=out_ap, in_=in_ap)
+            else:
+                nc.scalar.copy(out=out_ap, in_=in_ap)
+
+        def regroup_w(g):
+            gw = work.tile([P, 4 * C], BF16, name="gw", tag="gw", bufs=2, align_bytes=64)
+            state[("gw", g)] = gw
+            dst = gw[:].rearrange("p (c i t) -> p c t i", i=4, t=4)
+            src = w_raw[g][:].rearrange("p (t c i) -> p c t i", t=4, i=4)
+            n = W_GROUPS_ON_VECTOR
+            nc.vector.tensor_copy(out=dst[:, 0:n], in_=src[:, 0:n])
+            nc.scalar.copy(out=dst[:, n:128], in_=src[:, n:128])
+
+        def quant_w(g):
+            nc.vector.quantize_mx(
+                out=wq[:, C * g : C * (g + 1)].bitcast(FP8X4),
+                scales=ws[:, C * g : C * (g + 1)],
+                in_=state[("gw", g)][:],
+            )
+
+        def bias_transpose():
+            pb = ps_tp.tile([P, P], BF16, name="pb", tag="tp")
+            nc.tensor.transpose(out=pb[:], in_=b2rows[:], identity=identb[:])
+            state["pb"] = pb
+
+        def bias_evac():
+            nc.scalar.copy(out=b2col[:], in_=state["pb"][:, 0:4])
+
+        def transposes(u):
+            t, klen, k0 = pieces[u]
+            words = t[:].bitcast(F32)
+            w0 = (512 * (u % 4) - k0) // 2
+            for j in range(2):
+                xt = ps_tp.tile([P, 512], F32, name="xt", tag="tp")
+                state[("xt", u, j)] = xt
+                for tl in range(2):
+                    for uu in range(2):
+                        col = (2 * j + tl) * (klen // 2) + w0 + uu
+                        nc.tensor.transpose(
+                            out=xt[:, 256 * uu + P * tl : 256 * uu + P * (tl + 1)],
+                            in_=words[:, col : col + 2 * P - 1 : 2],
+                            identity=ident32[:],
+                        )
+
+        def evac(u, j, eng):
+            if j == 0:
+                state[("gh", u)] = work.tile([P, 4 * T], BF16, name="gh", tag="gh", bufs=4, align_bytes=64)
+            gh = state[("gh", u)]
+            copy_on(
+                eng,
+                gh[:].bitcast(F32)[:, 512 * j : 512 * (j + 1)].rearrange("p (n u) -> p n u", u=2),
+                state[("xt", u, j)][:].rearrange("p (u n) -> p n u", u=2),
+            )
+
+        def quant_h(u):
+            hq = work.tile([P, T], U32, name="hq", tag="hq", bufs=8, align_bytes=64)
+            hs = work.tile([P, T], U8, name="hs", tag="hs", bufs=8, align_bytes=64)
+            state[("hq", u)] = (hq, hs)
+            nc.vector.quantize_mx(out=hq[:].bitcast(FP8X4), scales=hs[:], in_=state[("gh", u)][:])
+
+        def mx_pass(b, ct, g):
+            n = state.get(("n", b, ct), 0)
+            if n == 0:
+                state[("acc", b, ct)] = ps_acc.tile([P, T], F32, name="acc", tag="acc")
+            state[("n", b, ct)] = n + 1
+            hq, hs = state[("hq", 4 * b + g)]
+            cols = slice(C * g + P * ct, C * g + P * (ct + 1))
+            nc.tensor.matmul_mx(
+                out=state[("acc", b, ct)][:],
+                lhsT=wq[:, cols].bitcast(FP8X4),
+                lhsT_scale=ws[:, cols],
+                rhs=hq[:].bitcast(FP8X4),
+                rhs_scale=hs[:],
+                start=(n == 0),
+                stop=(n == 3),
+            )
+
+        def unit_passes(u):
+            for ct in range(4):
+                mx_pass(u // 4, ct, u % 4)
+
+        def sigmoid(b, ct):
+            gt = work.tile([P, T], F32, name="gt", tag="gt", bufs=8)
+            state[("gt", b, ct)] = gt
+            nc.scalar.activation(
+                out=gt[:], in_=state[("acc", b, ct)][:], func=ACT.Sigmoid, bias=b2col[:, ct : ct + 1], scale=1.0
+            )
+
+        def memory_transposes():
+            for j in range(2):
+                pm = ps_tp.tile([P, 1024], BF16, name="pm", tag="tp")
+                for cl in range(2):
+                    for tt in range(4):
+                        nc.tensor.transpose(
+                            out=pm[:, 512 * cl + P * tt : 512 * cl + P * (tt + 1)],
+                            in_=mem_sb[:, C * tt + P * (2 * j + cl) : C * tt + P * (2 * j + cl + 1)],
+                            identity=identb[:],
+                        )
+                nc.scalar.mul(out=memq[:, 1024 * j : 1024 * (j + 1)], in_=pm[:], mul=-0.25)
+
+        def x_sums(b):
+            px = ps_tp.tile([P, P], F32, name="px", tag="tp")
+            for ct in range(4):
+                for j in range(4):
+                    nc.tensor.matmul(
+                        out=px[:, 32 * ct : 32 * (ct + 1)],
+                        lhsT=x_sb[b][:, C * j + P * ct : C * j + P * (ct + 1)],
+                        rhs=ones[:],
+                        start=(j == 0),
+                        stop=(j == 3),
+                    )
+            nc.scalar.mul(
+                out=xm4[b][:].rearrange("p (c o) -> p c o", o=1),
+                in_=px[:].rearrange("p (c n) -> p c n", n=32)[:, :, 0:1],
+                mul=1.0 / (4 * T),
+            )
+
+        def blend_mul(b, ct, lo=0, hi=T):
+            if lo == 0:
+                state[("pr", b, ct)] = work.tile([P, T], F32, name="pr", tag="pr", bufs=4)
+            nc.vector.scalar_tensor_tensor(
+                out=state[("pr", b, ct)][:, lo:hi], in0=memq[:, T * ct + lo : T * ct + hi],
+                scalar=xm4[b][:, ct : ct + 1], in1=state[("gt", b, ct)][:, lo:hi], op0=ALU.add, op1=ALU.mult,
+            )
+
+        def blend_sub(b, ct):
+            pr = state[("pr", b, ct)]
+            if b == 0:
+                nc.vector.scalar_tensor_tensor(
+                    out=acc_out[ct][:], in0=memq[:, T * ct : T * (ct + 1)], scalar=-4.0, in1=pr[:],
+                    op0=ALU.mult, op1=ALU.add,
+                )
+            else:
+                nc.vector.tensor_tensor(out=acc_out[ct][:], in0=acc_out[ct][:], in1=pr[:], op=ALU.add)
+
+        def blend_pair(b, c0, c1):
+            blend_mul(b, c0)
+            blend_mul(b, c1)
+            blend_sub(b, c0)
+            blend_sub(b, c1)
+
+        def finish_transposes(ct, src, first, last, t0=0, t1=4, pool=ps_tp, tag="tp"):
+            if first:
+                state[("pf", ct, t0)] = pool.tile([P, P * (t1 - t0)], F32, name="pf", tag=tag)
+            pf = state[("pf", ct, t0)]
+            for tt in range(t0, t1):
+                nc.tensor.matmul(
+                    out=pf[:, P * (tt - t0) : P * (tt - t0 + 1)], lhsT=src[:, P * tt : P * (tt + 1)], rhs=ident32[:],
+                    is_transpose=True, start=(first and tt == t0), stop=(last and tt == t1 - 1),
+                )
+
+        def finish_store(ct, t0=0, t1=4):
+            ot = work.tile([P, P * (t1 - t0)], F32, name="ot", tag="ot", bufs=5)
+            nc.scalar.copy(out=ot[:], in_=state[("pf", ct, t0)][:])
+            nc.sync.dma_start(
+                out=out[0].rearrange("(p t) c -> p t c", t=4)[:, t0:t1, P * ct : P * (ct + 1)],
+                in_=ot[:].rearrange("p (t c) -> p t c", t=t1 - t0),
+            )
+
+        def evacs(u, e0, e1):
+            evac(u, 0, e0)
+            evac(u, 1, e1)
+
+        regroup_w(0); quant_w(0)
+        transposes(0); evacs(0, "S", "V"); regroup_w(1); quant_h(0); quant_w(1)
+        transposes(1); evacs(1, "S", "V"); unit_passes(0); regroup_w(2); quant_h(1); quant_w(2)
+        transposes(2); evacs(2, "S", "V"); unit_passes(1); regroup_w(3); quant_h(2); quant_w(3)
+        transposes(3); bias_transpose(); evacs(3, "S", "V"); bias_evac(); unit_passes(2); quant_h(3)
+        transposes(4); transposes(5); evacs(4, "S", "V"); evacs(5, "S", "V")
+        unit_passes(3)
+        quant_h(4); quant_h(5)
+        sigmoid(0, 0); sigmoid(0, 1)
+        x_sums(0); memory_transposes()
+        sigmoid(0, 2); sigmoid(0, 3)
+        transposes(6); transposes(7)
+        blend_pair(0, 0, 1)
+        evacs(6, "S", "S"); evacs(7, "S", "S")
+        for ct in range(4):
+            mx_pass(1, ct, 0)
+        quant_h(6); quant_h(7)
+        transposes(8); transposes(9)
+        blend_pair(0, 2, 3)
+        evacs(8, "S", "S"); evacs(9, "S", "S")
+        for ct in (0, 1):
+            mx_pass(1, ct, 1); mx_pass(1, ct, 2); mx_pass(1, ct, 3); sigmoid(1, ct)
+        quant_h(8); quant_h(9)
+        x_sums(1)
+        transposes(10); transposes(11); evacs(10, "S", "S"); evacs(11, "S", "S")
+        blend_pair(1, 0, 1)
+        for ct in (2, 3):
+            mx_pass(1, ct, 1); mx_pass(1, ct, 2); mx_pass(1, ct, 3); sigmoid(1, ct)
+        quant_h(10); quant_h(11)
+        transposes(12); transposes(13); evacs(12, "S", "S"); evacs(13, "S", "S")
+        blend_pair(1, 2, 3)
+        for ct in (0, 1):
+            for g in range(4):
+                mx_pass(2, ct, g)
+            sigmoid(2, ct)
+        quant_h(12); quant_h(13)
+        x_sums(2)
+        transposes(14); transposes(15); evacs(14, "S", "S"); evacs(15, "S", "S")
+        blend_pair(2, 0, 1)
+        for ct in (2, 3):
+            for g in range(4):
+                mx_pass(2, ct, g)
+            sigmoid(2, ct)
+        quant_h(14); quant_h(15)
+        x_sums(3)
+        blend_pair(2, 2, 3)
+        for ct in range(4):
+            for g in range(4):
+                mx_pass(3, ct, g)
+            sigmoid(3, ct)
+        finish_transposes(2, acc_out[2], True, False)
+        finish_transposes(3, acc_out[3], True, False, 0, 2)
+        finish_transposes(3, acc_out[3], True, False, 2, 4, ps_acc, "acc")
+        blend_pair(3, 0, 1)
+        finish_transposes(0, acc_out[0], True, True); finish_store(0)
+        finish_transposes(1, acc_out[1], True, True); finish_store(1)
+        blend_mul(3, 2)
+        finish_transposes(2, state[("pr", 3, 2)], False, True); finish_store(2)
+        blend_mul(3, 3, 0, 256)
+        finish_transposes(3, state[("pr", 3, 3)], False, True, 0, 2); finish_store(3, 0, 2)
+        blend_mul(3, 3, 256, 512)
+        finish_transposes(3, state[("pr", 3, 3)], False, True, 2, 4); finish_store(3, 2, 4)

@@ -20,7 +20,8 @@ C = 512
 F = 2048
 FLOPS = 2 * B * T * F * C
 
-W_GROUPS_ON_VECTOR = 84
+W_GROUPS_ON_VECTOR = 64
+NX = 32
 
 
 def tile_dynamicmemorybank_pb_kernel(tc, h, x, memory, w2, b2, out):
@@ -35,7 +36,7 @@ def tile_dynamicmemorybank_pb_kernel(tc, h, x, memory, w2, b2, out):
 
         ident32 = const.tile([P, P], F32, name="ident32")
         identb = const.tile([P, P], BF16, name="identb")
-        ones = const.tile([P, 32], BF16, name="ones")
+        ones = const.tile([P, NX], BF16, name="ones")
         b2rows = const.tile([P, P], BF16, name="b2rows")
         b2col = const.tile([P, 4], F32, name="b2col")
         warm = const.tile([P, 2], F32, name="warm")
@@ -48,48 +49,54 @@ def tile_dynamicmemorybank_pb_kernel(tc, h, x, memory, w2, b2, out):
         nc.scalar.activation(out=warm[:, 1:2], in_=warm[:, 0:1], func=ACT.Sigmoid)
 
         w_raw = [keep.tile([P, 4 * C], BF16, name="w_raw%d" % g) for g in range(4)]
-        pieces = {}
         x_sb = [keep.tile([P, 4 * C], BF16, name="x_sb%d" % b) for b in range(B)]
         mem_sb = keep.tile([P, 4 * C], BF16, name="mem_sb")
+        pieces = {}
 
         def load_w(g):
             nc.sync.dma_start(
-                out=w_raw[g][:],
-                in_=w2[512 * g : 512 * (g + 1), :].rearrange("(p j) c -> p (j c)", j=4),
+                out=w_raw[g][:], in_=w2[512 * g : 512 * (g + 1), :].rearrange("(p j) c -> p (j c)", j=4)
             )
 
-        def load_h(b, k0, klen):
-            t = keep.tile([P, 4 * klen], BF16, name="h_%d_%d" % (b, k0))
+        def load_h(b, k0, klen, t0=0, t1=4):
+            t = keep.tile([P, (t1 - t0) * klen], BF16, name="h_%d_%d_%d" % (b, k0, t0))
             nc.sync.dma_start(
-                out=t[:].rearrange("p (t k) -> p t k", t=4),
-                in_=h[b].rearrange("(p t) k -> p t k", t=4)[:, :, k0 : k0 + klen],
+                out=t[:].rearrange("p (t k) -> p t k", t=t1 - t0),
+                in_=h[b].rearrange("(p t) k -> p t k", t=4)[:, t0:t1, k0 : k0 + klen],
             )
             for g in range(k0 // 512, (k0 + klen) // 512):
-                pieces[4 * b + g] = (t, klen, k0)
+                for j in range(t0 // 2, t1 // 2):
+                    pieces[(4 * b + g, j)] = (t, klen, k0, t0)
 
         def load_x(b):
             nc.sync.dma_start(out=x_sb[b][:], in_=x[b].rearrange("(p j) c -> p (j c)", j=4))
 
-        for g in range(4):
-            load_w(g)
-            load_h(0, 512 * g, 512)
-        load_h(1, 0, 1024)
+        load_h(0, 0, 512, 0, 2)
+        load_h(0, 0, 512, 2, 4)
+        load_w(0)
+        load_h(0, 512, 512)
+        load_w(1)
+        load_h(0, 1024, 512)
+        load_w(2)
+        load_h(0, 1536, 512)
+        load_w(3)
+        load_h(1, 0, 512)
+        load_h(1, 512, 512)
+        load_h(1, 1024, 1024)
         nc.sync.dma_start(out=mem_sb[:], in_=memory[0].rearrange("(p t) c -> p (t c)", t=4))
         load_x(0)
-        load_h(1, 1024, 1024)
-        load_h(2, 0, 1024)
         load_x(1)
+        load_h(2, 0, 1024)
         load_h(2, 1024, 1024)
-        load_h(3, 0, 1024)
         load_x(2)
-        load_h(3, 1024, 1024)
         load_x(3)
+        load_h(3, 0, 1024)
+        load_h(3, 1024, 1024)
 
         wq = keep.tile([P, 4 * C], U32, name="wq", align_bytes=64)
         ws = keep.tile([P, 4 * C], U8, name="ws", align_bytes=64)
         memq = keep.tile([P, 4 * T], BF16, name="memq")
-        acc_out = [keep.tile([P, T], F32, name="acc_out%d" % ct) for ct in range(4)]
-        xm4 = [keep.tile([P, 4], F32, name="xm4_%d" % b) for b in range(B)]
+        xm4 = [keep.tile([P, 8], F32, name="xm4_%d" % i) for i in range(2)]
 
         state = {}
 
@@ -118,25 +125,33 @@ def tile_dynamicmemorybank_pb_kernel(tc, h, x, memory, w2, b2, out):
         def bias_transpose():
             pb = ps_tp.tile([P, P], BF16, name="pb", tag="tp")
             nc.tensor.transpose(out=pb[:], in_=b2rows[:], identity=identb[:])
-            state["pb"] = pb
+            nc.scalar.copy(out=b2col[:], in_=pb[:, 0:4])
 
-        def bias_evac():
-            nc.scalar.copy(out=b2col[:], in_=state["pb"][:, 0:4])
+        def split_words(u):
+            t, klen, k0, t0 = pieces[(u, 0)]
+            w0 = (512 * (u % 4) - k0) // 2
+            hp = work.tile([P, 1024], F32, name="hp", tag="hp", bufs=4)
+            state[("hp", u)] = hp
+            nc.vector.tensor_copy(
+                out=hp[:].rearrange("p (t u w) -> p t u w", t=4, u=2),
+                in_=t[:].bitcast(F32).rearrange("p (t k) -> p t k", t=4)[:, :, w0 : w0 + 256].rearrange("p t (w u) -> p t u w", u=2),
+            )
 
         def transposes(u):
-            t, klen, k0 = pieces[u]
-            words = t[:].bitcast(F32)
-            w0 = (512 * (u % 4) - k0) // 2
             for j in range(2):
                 xt = ps_tp.tile([P, 512], F32, name="xt", tag="tp")
                 state[("xt", u, j)] = xt
                 for tl in range(2):
                     for uu in range(2):
-                        col = (2 * j + tl) * (klen // 2) + w0 + uu
+                        if ("hp", u) in state:
+                            col = 256 * (2 * j + tl) + P * uu
+                            src = state[("hp", u)][:, col : col + P]
+                        else:
+                            t, klen, k0, t0 = pieces[(u, j)]
+                            col = (2 * j + tl - t0) * (klen // 2) + (512 * (u % 4) - k0) // 2 + uu
+                            src = t[:].bitcast(F32)[:, col : col + 2 * P - 1 : 2]
                         nc.tensor.transpose(
-                            out=xt[:, 256 * uu + P * tl : 256 * uu + P * (tl + 1)],
-                            in_=words[:, col : col + 2 * P - 1 : 2],
-                            identity=ident32[:],
+                            out=xt[:, 256 * uu + P * tl : 256 * uu + P * (tl + 1)], in_=src, identity=ident32[:]
                         )
 
         def evac(u, j, eng):
@@ -149,18 +164,23 @@ def tile_dynamicmemorybank_pb_kernel(tc, h, x, memory, w2, b2, out):
                 state[("xt", u, j)][:].rearrange("p (u n) -> p n u", u=2),
             )
 
+        def evacs(u, e0, e1):
+            evac(u, 0, e0)
+            evac(u, 1, e1)
+
         def quant_h(u):
             hq = work.tile([P, T], U32, name="hq", tag="hq", bufs=8, align_bytes=64)
             hs = work.tile([P, T], U8, name="hs", tag="hs", bufs=8, align_bytes=64)
             state[("hq", u)] = (hq, hs)
             nc.vector.quantize_mx(out=hq[:].bitcast(FP8X4), scales=hs[:], in_=state[("gh", u)][:])
 
-        def mx_pass(b, ct, g):
+        def mx_pass(u, ct):
+            b, g = u // 4, u % 4
             n = state.get(("n", b, ct), 0)
             if n == 0:
                 state[("acc", b, ct)] = ps_acc.tile([P, T], F32, name="acc", tag="acc")
             state[("n", b, ct)] = n + 1
-            hq, hs = state[("hq", 4 * b + g)]
+            hq, hs = state[("hq", u)]
             cols = slice(C * g + P * ct, C * g + P * (ct + 1))
             nc.tensor.matmul_mx(
                 out=state[("acc", b, ct)][:],
@@ -172,16 +192,21 @@ def tile_dynamicmemorybank_pb_kernel(tc, h, x, memory, w2, b2, out):
                 stop=(n == 3),
             )
 
-        def unit_passes(u):
+        def passes(u):
             for ct in range(4):
-                mx_pass(u // 4, ct, u % 4)
+                mx_pass(u, ct)
 
-        def sigmoid(b, ct):
-            gt = work.tile([P, T], F32, name="gt", tag="gt", bufs=8)
-            state[("gt", b, ct)] = gt
+        def sigmoid(b, ct, lo=0, hi=T):
+            if lo == 0:
+                state[("gt", b, ct)] = keep.tile([P, T], F32, name="gt_%d_%d" % (b, ct))
             nc.scalar.activation(
-                out=gt[:], in_=state[("acc", b, ct)][:], func=ACT.Sigmoid, bias=b2col[:, ct : ct + 1], scale=1.0
+                out=state[("gt", b, ct)][:, lo:hi], in_=state[("acc", b, ct)][:, lo:hi], func=ACT.Sigmoid,
+                bias=b2col[:, ct : ct + 1], scale=1.0,
             )
+
+        def sigmoids(b):
+            for ct in range(4):
+                sigmoid(b, ct)
 
         def memory_transposes():
             for j in range(2):
@@ -193,130 +218,121 @@ def tile_dynamicmemorybank_pb_kernel(tc, h, x, memory, w2, b2, out):
                             in_=mem_sb[:, C * tt + P * (2 * j + cl) : C * tt + P * (2 * j + cl + 1)],
                             identity=identb[:],
                         )
-                nc.scalar.mul(out=memq[:, 1024 * j : 1024 * (j + 1)], in_=pm[:], mul=-0.25)
+                state[("pm", j)] = pm
 
-        def x_sums(b):
-            px = ps_tp.tile([P, P], F32, name="px", tag="tp")
-            for ct in range(4):
-                for j in range(4):
-                    nc.tensor.matmul(
-                        out=px[:, 32 * ct : 32 * (ct + 1)],
-                        lhsT=x_sb[b][:, C * j + P * ct : C * j + P * (ct + 1)],
-                        rhs=ones[:],
-                        start=(j == 0),
-                        stop=(j == 3),
-                    )
+        def memory_evac(j):
+            nc.scalar.mul(out=memq[:, 1024 * j : 1024 * (j + 1)], in_=state[("pm", j)][:], mul=-0.25)
+
+        def x_sums(i):
+            px = ps_tp.tile([P, 8 * NX], F32, name="px", tag="tp")
+            for bl in range(2):
+                for ct in range(4):
+                    for j in range(4):
+                        nc.tensor.matmul(
+                            out=px[:, NX * (4 * bl + ct) : NX * (4 * bl + ct + 1)],
+                            lhsT=x_sb[2 * i + bl][:, C * j + P * ct : C * j + P * (ct + 1)],
+                            rhs=ones[:],
+                            start=(j == 0),
+                            stop=(j == 3),
+                        )
             nc.scalar.mul(
-                out=xm4[b][:].rearrange("p (c o) -> p c o", o=1),
-                in_=px[:].rearrange("p (c n) -> p c n", n=32)[:, :, 0:1],
+                out=xm4[i][:].rearrange("p (c o) -> p c o", o=1),
+                in_=px[:].rearrange("p (c n) -> p c n", n=NX)[:, :, 0:1],
                 mul=1.0 / (4 * T),
             )
 
-        def blend_mul(b, ct, lo=0, hi=T):
-            if lo == 0:
-                state[("pr", b, ct)] = work.tile([P, T], F32, name="pr", tag="pr", bufs=4)
+        def blend(b, ct, lo=0, hi=T):
+            gt = state[("gt", b, ct)]
             nc.vector.scalar_tensor_tensor(
-                out=state[("pr", b, ct)][:, lo:hi], in0=memq[:, T * ct + lo : T * ct + hi],
-                scalar=xm4[b][:, ct : ct + 1], in1=state[("gt", b, ct)][:, lo:hi], op0=ALU.add, op1=ALU.mult,
+                out=gt[:, lo:hi], in0=memq[:, T * ct + lo : T * ct + hi],
+                scalar=xm4[b // 2][:, 4 * (b % 2) + ct : 4 * (b % 2) + ct + 1], in1=gt[:, lo:hi],
+                op0=ALU.add, op1=ALU.mult,
             )
 
-        def blend_sub(b, ct):
-            pr = state[("pr", b, ct)]
-            if b == 0:
-                nc.vector.scalar_tensor_tensor(
-                    out=acc_out[ct][:], in0=memq[:, T * ct : T * (ct + 1)], scalar=-4.0, in1=pr[:],
-                    op0=ALU.mult, op1=ALU.add,
-                )
-            else:
-                nc.vector.tensor_tensor(out=acc_out[ct][:], in0=acc_out[ct][:], in1=pr[:], op=ALU.add)
+        def add_up(b, ct):
+            t0, t1 = state[("gt", 0, ct)], state[("gt", b, ct)]
+            nc.vector.tensor_tensor(out=t0[:], in0=t0[:], in1=t1[:], op=ALU.add)
 
-        def blend_pair(b, c0, c1):
-            blend_mul(b, c0)
-            blend_mul(b, c1)
-            blend_sub(b, c0)
-            blend_sub(b, c1)
+        def add_memory(ct):
+            gt = state[("gt", 0, ct)]
+            nc.vector.scalar_tensor_tensor(
+                out=gt[:], in0=memq[:, T * ct : T * (ct + 1)], scalar=-4.0, in1=gt[:], op0=ALU.mult, op1=ALU.add
+            )
 
-        def finish_transposes(ct, src, first, last, t0=0, t1=4, pool=ps_tp, tag="tp"):
+        def sum_part(ct, b, first, last, t0=0, t1=4):
             if first:
-                state[("pf", ct, t0)] = pool.tile([P, P * (t1 - t0)], F32, name="pf", tag=tag)
+                state[("pf", ct, t0)] = ps_tp.tile([P, P * (t1 - t0)], F32, name="pf", tag="tp")
             pf = state[("pf", ct, t0)]
+            src = state[("gt", b, ct)]
             for tt in range(t0, t1):
                 nc.tensor.matmul(
                     out=pf[:, P * (tt - t0) : P * (tt - t0 + 1)], lhsT=src[:, P * tt : P * (tt + 1)], rhs=ident32[:],
                     is_transpose=True, start=(first and tt == t0), stop=(last and tt == t1 - 1),
                 )
 
-        def finish_store(ct, t0=0, t1=4):
+        def store(ct, eng, t0=0, t1=4):
             ot = work.tile([P, P * (t1 - t0)], F32, name="ot", tag="ot", bufs=5)
-            nc.scalar.copy(out=ot[:], in_=state[("pf", ct, t0)][:])
+            if eng == "S":
+                nc.scalar.copy(out=ot[:], in_=state[("pf", ct, t0)][:])
+            else:
+                nc.vector.tensor_tensor(
+                    out=ot[:].rearrange("p (t c) -> p t c", t=t1 - t0),
+                    in0=state[("pf", ct, t0)][:].rearrange("p (t c) -> p t c", t=t1 - t0),
+                    in1=mem_sb[:].rearrange("p (t c) -> p t c", t=4)[:, t0:t1, P * ct : P * (ct + 1)],
+                    op=ALU.add,
+                )
             nc.sync.dma_start(
                 out=out[0].rearrange("(p t) c -> p t c", t=4)[:, t0:t1, P * ct : P * (ct + 1)],
                 in_=ot[:].rearrange("p (t c) -> p t c", t=t1 - t0),
             )
 
-        def evacs(u, e0, e1):
-            evac(u, 0, e0)
-            evac(u, 1, e1)
-
-        regroup_w(0); quant_w(0)
-        transposes(0); evacs(0, "S", "V"); regroup_w(1); quant_h(0); quant_w(1)
-        transposes(1); evacs(1, "S", "V"); unit_passes(0); regroup_w(2); quant_h(1); quant_w(2)
-        transposes(2); evacs(2, "S", "V"); unit_passes(1); regroup_w(3); quant_h(2); quant_w(3)
-        transposes(3); bias_transpose(); evacs(3, "S", "V"); bias_evac(); unit_passes(2); quant_h(3)
-        transposes(4); transposes(5); evacs(4, "S", "V"); evacs(5, "S", "V")
-        unit_passes(3)
-        quant_h(4); quant_h(5)
-        sigmoid(0, 0); sigmoid(0, 1)
-        x_sums(0); memory_transposes()
-        sigmoid(0, 2); sigmoid(0, 3)
-        transposes(6); transposes(7)
-        blend_pair(0, 0, 1)
-        evacs(6, "S", "S"); evacs(7, "S", "S")
-        for ct in range(4):
-            mx_pass(1, ct, 0)
-        quant_h(6); quant_h(7)
-        transposes(8); transposes(9)
-        blend_pair(0, 2, 3)
-        evacs(8, "S", "S"); evacs(9, "S", "S")
-        for ct in (0, 1):
-            mx_pass(1, ct, 1); mx_pass(1, ct, 2); mx_pass(1, ct, 3); sigmoid(1, ct)
-        quant_h(8); quant_h(9)
-        x_sums(1)
+        transposes(0); evacs(0, "S", "S"); regroup_w(0)
+        quant_h(0); quant_w(0)
+        transposes(1); evacs(1, "S", "V"); regroup_w(1); quant_h(1); quant_w(1)
+        passes(0)
+        transposes(2); evacs(2, "S", "V"); regroup_w(2); quant_h(2); quant_w(2)
+        passes(1)
+        transposes(3); evacs(3, "S", "V"); regroup_w(3); split_words(4); quant_h(3); split_words(5); quant_w(3)
+        passes(2)
+        bias_transpose()
+        transposes(4); transposes(5); evacs(4, "S", "S"); evacs(5, "S", "S")
+        split_words(6); quant_h(4); split_words(7); quant_h(5)
+        passes(3); sigmoids(0)
+        transposes(6); transposes(7); evacs(6, "V", "S"); evacs(7, "V", "S")
+        passes(4); passes(5)
+        quant_h(6); split_words(8); quant_h(7); split_words(9)
+        memory_transposes(); memory_evac(0); memory_evac(1)
+        x_sums(0)
+        transposes(8); transposes(9); evacs(8, "S", "S"); evacs(9, "S", "S")
+        split_words(10); blend(0, 0); split_words(11); quant_h(8); blend(0, 1); quant_h(9); blend(0, 2)
+        passes(6); passes(7); sigmoids(1)
         transposes(10); transposes(11); evacs(10, "S", "S"); evacs(11, "S", "S")
-        blend_pair(1, 0, 1)
-        for ct in (2, 3):
-            mx_pass(1, ct, 1); mx_pass(1, ct, 2); mx_pass(1, ct, 3); sigmoid(1, ct)
-        quant_h(10); quant_h(11)
+        split_words(12); blend(0, 3); split_words(13); blend(1, 0); quant_h(10); blend(1, 1); quant_h(11)
+        passes(8); passes(9)
+        x_sums(1)
         transposes(12); transposes(13); evacs(12, "S", "S"); evacs(13, "S", "S")
-        blend_pair(1, 2, 3)
-        for ct in (0, 1):
-            for g in range(4):
-                mx_pass(2, ct, g)
-            sigmoid(2, ct)
-        quant_h(12); quant_h(13)
-        x_sums(2)
-        transposes(14); transposes(15); evacs(14, "S", "S"); evacs(15, "S", "S")
-        blend_pair(2, 0, 1)
-        for ct in (2, 3):
-            for g in range(4):
-                mx_pass(2, ct, g)
-            sigmoid(2, ct)
-        quant_h(14); quant_h(15)
-        x_sums(3)
-        blend_pair(2, 2, 3)
-        for ct in range(4):
-            for g in range(4):
-                mx_pass(3, ct, g)
+        split_words(14); split_words(15); add_memory(0); quant_h(12); add_memory(1); quant_h(13); blend(1, 2); blend(1, 3)
+        passes(10); passes(11); sigmoids(2)
+        transposes(14); transposes(15); evacs(14, "V", "S"); evacs(15, "S", "S")
+        blend(2, 0); blend(2, 1); quant_h(14); blend(2, 2); quant_h(15)
+        passes(12); passes(13)
+        blend(2, 3); add_up(1, 3); add_up(2, 3)
+        for ct in range(3):
+            mx_pass(14, ct)
+            mx_pass(15, ct)
             sigmoid(3, ct)
-        finish_transposes(2, acc_out[2], True, False)
-        finish_transposes(3, acc_out[3], True, False, 0, 2)
-        finish_transposes(3, acc_out[3], True, False, 2, 4, ps_acc, "acc")
-        blend_pair(3, 0, 1)
-        finish_transposes(0, acc_out[0], True, True); finish_store(0)
-        finish_transposes(1, acc_out[1], True, True); finish_store(1)
-        blend_mul(3, 2)
-        finish_transposes(2, state[("pr", 3, 2)], False, True); finish_store(2)
-        blend_mul(3, 3, 0, 256)
-        finish_transposes(3, state[("pr", 3, 3)], False, True, 0, 2); finish_store(3, 0, 2)
-        blend_mul(3, 3, 256, 512)
-        finish_transposes(3, state[("pr", 3, 3)], False, True, 2, 4); finish_store(3, 2, 4)
+        mx_pass(14, 3); mx_pass(15, 3); sigmoid(3, 3, 0, 256); sigmoid(3, 3, 256, 512)
+        for b in range(3):
+            sum_part(0, b, b == 0, False)
+        for b in range(3):
+            sum_part(1, b, b == 0, False)
+        blend(3, 0); sum_part(0, 3, False, True); store(0, "S")
+        for b in range(3):
+            sum_part(2, b, b == 0, False)
+        blend(3, 1); sum_part(1, 3, False, True); store(1, "S")
+        sum_part(3, 0, True, False, 0, 2)
+        blend(3, 2); sum_part(2, 3, False, True)
+        blend(3, 3, 0, 256); blend(3, 3, 256, 512); store(2, "V")
+        sum_part(3, 3, False, True, 0, 2); store(3, "V", 0, 2)
+        sum_part(3, 0, True, False, 2, 4)
+        sum_part(3, 3, False, True, 2, 4); store(3, "V", 2, 4)

@@ -40,6 +40,8 @@ def tile_dynamicmemorybank_pb_kernel(tc, h, x, memory, w2, b2, out):
         b2rows = const.tile([P, P], BF16, name="b2rows")
         b2col = const.tile([P, 4], F32, name="b2col")
         warm = const.tile([P, 2], F32, name="warm")
+        idle = const.tile([P, T], BF16, name="idle")
+        nc.vector.memset(idle[:], 0.0)
         make_identity(nc, ident32[:])
         make_identity(nc, identb[:])
         nc.vector.memset(b2rows[:], 0.0)
@@ -121,6 +123,11 @@ def tile_dynamicmemorybank_pb_kernel(tc, h, x, memory, w2, b2, out):
                 scales=ws[:, C * g : C * (g + 1)],
                 in_=state[("gw", g)][:],
             )
+
+        def keep_clock(n):
+            pw = ps_acc.tile([P, T], F32, name="pw", tag="acc")
+            for i in range(n):
+                nc.tensor.matmul(out=pw[:], lhsT=idle[:, 0:P], rhs=idle[:], start=True, stop=True)
 
         def bias_transpose():
             pb = ps_tp.tile([P, P], BF16, name="pb", tag="tp")
@@ -286,8 +293,10 @@ def tile_dynamicmemorybank_pb_kernel(tc, h, x, memory, w2, b2, out):
                 in_=ot[:].rearrange("p (t c) -> p t c", t=t1 - t0),
             )
 
+        keep_clock(5)
         transposes(0); evacs(0, "S", "S"); regroup_w(0)
         quant_h(0); quant_w(0)
+        keep_clock(3)
         transposes(1); evacs(1, "S", "V"); regroup_w(1); quant_h(1); quant_w(1)
         passes(0)
         transposes(2); evacs(2, "S", "V"); regroup_w(2); quant_h(2); quant_w(2)

@@ -20,7 +20,7 @@ C = 512
 F = 2048
 FLOPS = 2 * B * T * F * C
 
-W_GROUPS_ON_VECTOR = 64
+W_GROUPS_ON_VECTOR = 84
 NX = 32
 
 
@@ -60,40 +60,35 @@ def tile_dynamicmemorybank_pb_kernel(tc, h, x, memory, w2, b2, out):
                 out=w_raw[g][:], in_=w2[512 * g : 512 * (g + 1), :].rearrange("(p j) c -> p (j c)", j=4)
             )
 
-        def load_h(b, k0, klen, t0=0, t1=4):
-            t = keep.tile([P, (t1 - t0) * klen], BF16, name="h_%d_%d_%d" % (b, k0, t0))
+        def load_h(b, t0, t1):
+            ht = keep.tile([P, (t1 - t0) * F], BF16, name="h_%d_%d" % (b, t0))
             nc.sync.dma_start(
-                out=t[:].rearrange("p (t k) -> p t k", t=t1 - t0),
-                in_=h[b].rearrange("(p t) k -> p t k", t=4)[:, t0:t1, k0 : k0 + klen],
+                out=ht[:].rearrange("p (t k) -> p t k", t=t1 - t0), in_=h[b].rearrange("(p t) k -> p t k", t=4)[:, t0:t1, :]
             )
-            for g in range(k0 // 512, (k0 + klen) // 512):
-                for j in range(t0 // 2, t1 // 2):
-                    pieces[(4 * b + g, j)] = (t, klen, k0, t0)
+            for t in range(t0, t1):
+                pieces[(b, t)] = ht[:].bitcast(F32)[:, (F // 2) * (t - t0) : (F // 2) * (t - t0 + 1)]
 
         def load_x(b):
             nc.sync.dma_start(out=x_sb[b][:], in_=x[b].rearrange("(p j) c -> p (j c)", j=4))
 
-        load_h(0, 0, 512, 0, 2)
-        load_h(0, 0, 512, 2, 4)
+        for t in range(4):
+            load_h(0, t, t + 1)
         load_w(0)
-        load_h(0, 512, 512)
         load_w(1)
-        load_h(0, 1024, 512)
+        load_h(1, 0, 1)
+        load_h(1, 1, 2)
         load_w(2)
-        load_h(0, 1536, 512)
         load_w(3)
-        load_h(1, 0, 512)
-        load_h(1, 512, 512)
-        load_h(1, 1024, 1024)
+        load_h(1, 2, 4)
         nc.sync.dma_start(out=mem_sb[:], in_=memory[0].rearrange("(p t) c -> p (t c)", t=4))
+        load_h(2, 0, 2)
         load_x(0)
         load_x(1)
-        load_h(2, 0, 1024)
-        load_h(2, 1024, 1024)
+        load_h(2, 2, 4)
+        load_h(3, 0, 2)
         load_x(2)
         load_x(3)
-        load_h(3, 0, 1024)
-        load_h(3, 1024, 1024)
+        load_h(3, 2, 4)
 
         wq = keep.tile([P, 4 * C], U32, name="wq", align_bytes=64)
         ws = keep.tile([P, 4 * C], U8, name="ws", align_bytes=64)
@@ -134,74 +129,95 @@ def tile_dynamicmemorybank_pb_kernel(tc, h, x, memory, w2, b2, out):
             nc.tensor.transpose(out=pb[:], in_=b2rows[:], identity=identb[:])
             nc.scalar.copy(out=b2col[:], in_=pb[:, 0:4])
 
-        def split_words(u):
-            t, klen, k0, t0 = pieces[(u, 0)]
-            w0 = (512 * (u % 4) - k0) // 2
-            hp = work.tile([P, 1024], F32, name="hp", tag="hp", bufs=4)
-            state[("hp", u)] = hp
-            nc.vector.tensor_copy(
-                out=hp[:].rearrange("p (t u w) -> p t u w", t=4, u=2),
-                in_=t[:].bitcast(F32).rearrange("p (t k) -> p t k", t=4)[:, :, w0 : w0 + 256].rearrange("p t (w u) -> p t u w", u=2),
-            )
-
-        def transposes(u):
-            for j in range(2):
-                xt = ps_tp.tile([P, 512], F32, name="xt", tag="tp")
-                state[("xt", u, j)] = xt
-                for tl in range(2):
-                    for uu in range(2):
-                        if ("hp", u) in state:
-                            col = 256 * (2 * j + tl) + P * uu
-                            src = state[("hp", u)][:, col : col + P]
-                        else:
-                            t, klen, k0, t0 = pieces[(u, j)]
-                            col = (2 * j + tl - t0) * (klen // 2) + (512 * (u % 4) - k0) // 2 + uu
-                            src = t[:].bitcast(F32)[:, col : col + 2 * P - 1 : 2]
-                        nc.tensor.transpose(
-                            out=xt[:, 256 * uu + P * tl : 256 * uu + P * (tl + 1)], in_=src, identity=ident32[:]
-                        )
-
-        def evac(u, j, eng):
-            if j == 0:
-                state[("gh", u)] = work.tile([P, 4 * T], BF16, name="gh", tag="gh", bufs=4, align_bytes=64)
-            gh = state[("gh", u)]
+        def split_words(b, t, eng="V"):
+            hp = work.tile([P, F // 2], F32, name="hp", tag="hp", bufs=4)
+            state[("hp", b, t)] = hp
             copy_on(
                 eng,
-                gh[:].bitcast(F32)[:, 512 * j : 512 * (j + 1)].rearrange("p (n u) -> p n u", u=2),
-                state[("xt", u, j)][:].rearrange("p (u n) -> p n u", u=2),
+                hp[:].rearrange("p (g u w) -> p g u w", g=4, u=2),
+                pieces[(b, t)].rearrange("p (g w u) -> p g u w", g=4, u=2),
             )
 
-        def evacs(u, e0, e1):
-            evac(u, 0, e0)
-            evac(u, 1, e1)
+        def transposes(b, tp, by_token=False):
+            xt = [ps_tp.tile([P, 512], F32, name="xt", tag="tp") for g in range(4)]
+            state[("xt", b, tp)] = xt
+            runs = [(g, tl) for tl in range(2) for g in range(4)] if by_token else [(g, tl) for g in range(4) for tl in range(2)]
+            for g, tl in runs:
+                for u in range(2):
+                    t = 2 * tp + tl
+                    if ("hp", b, t) in state:
+                        src = state[("hp", b, t)][:, 256 * g + P * u : 256 * g + P * (u + 1)]
+                    else:
+                        src = pieces[(b, t)][:, 256 * g + u : 256 * (g + 1) + u - 1 : 2]
+                    nc.tensor.transpose(out=xt[g][:, 256 * u + P * tl : 256 * u + P * (tl + 1)], in_=src, identity=ident32[:])
 
-        def quant_h(u):
-            hq = work.tile([P, T], U32, name="hq", tag="hq", bufs=8, align_bytes=64)
-            hs = work.tile([P, T], U8, name="hs", tag="hs", bufs=8, align_bytes=64)
-            state[("hq", u)] = (hq, hs)
-            nc.vector.quantize_mx(out=hq[:].bitcast(FP8X4), scales=hs[:], in_=state[("gh", u)][:])
+        def evac(b, tp, g, eng):
+            if g == 0:
+                state[("gh", b, tp)] = work.tile([P, 4096], BF16, name="gh", tag="gh", bufs=3, align_bytes=64)
+            gh = state[("gh", b, tp)]
+            copy_on(
+                eng,
+                gh[:].bitcast(F32)[:, 512 * g : 512 * (g + 1)].rearrange("p (n u) -> p n u", u=2),
+                state[("xt", b, tp)][g][:].rearrange("p (u n) -> p n u", u=2),
+            )
 
-        def mx_pass(u, ct):
-            b, g = u // 4, u % 4
-            n = state.get(("n", b, ct), 0)
-            if n == 0:
+        def evacs(b, tp, engs):
+            for g in range(4):
+                evac(b, tp, g, engs[g])
+
+        def quant_first(tp, g):
+            if tp == 0 and g == 0:
+                state[("hq", 0)] = (
+                    keep.tile([P, 4 * T], U32, name="hq0", align_bytes=64), keep.tile([P, 4 * T], U8, name="hs0", align_bytes=64)
+                )
+            hq, hs = state[("hq", 0)]
+            c0 = T * g + 256 * tp
+            nc.vector.quantize_mx(
+                out=hq[:, c0 : c0 + 256].bitcast(FP8X4), scales=hs[:, c0 : c0 + 256],
+                in_=state[("gh", 0, tp)][:, 1024 * g : 1024 * (g + 1)],
+            )
+
+        def quant(b, tp, gp):
+            if gp == 0:
+                state[("hq", b, tp)] = (
+                    work.tile([P, 1024], U32, name="hq", tag="hq", bufs=3, align_bytes=64),
+                    work.tile([P, 1024], U8, name="hs", tag="hs", bufs=3, align_bytes=64),
+                )
+            hq, hs = state[("hq", b, tp)]
+            nc.vector.quantize_mx(
+                out=hq[:, 512 * gp : 512 * (gp + 1)].bitcast(FP8X4), scales=hs[:, 512 * gp : 512 * (gp + 1)],
+                in_=state[("gh", b, tp)][:, 2048 * gp : 2048 * (gp + 1)],
+            )
+
+        def accumulator(b, ct):
+            if ("acc", b, ct) not in state:
                 state[("acc", b, ct)] = ps_acc.tile([P, T], F32, name="acc", tag="acc")
-            state[("n", b, ct)] = n + 1
-            hq, hs = state[("hq", u)]
-            cols = slice(C * g + P * ct, C * g + P * (ct + 1))
-            nc.tensor.matmul_mx(
-                out=state[("acc", b, ct)][:],
-                lhsT=wq[:, cols].bitcast(FP8X4),
-                lhsT_scale=ws[:, cols],
-                rhs=hq[:].bitcast(FP8X4),
-                rhs_scale=hs[:],
-                start=(n == 0),
-                stop=(n == 3),
-            )
+            return state[("acc", b, ct)]
 
-        def passes(u):
+        def first_passes(g):
+            hq, hs = state[("hq", 0)]
             for ct in range(4):
-                mx_pass(u, ct)
+                cols = slice(C * g + P * ct, C * g + P * (ct + 1))
+                nc.tensor.matmul_mx(
+                    out=accumulator(0, ct)[:], lhsT=wq[:, cols].bitcast(FP8X4), lhsT_scale=ws[:, cols],
+                    rhs=hq[:, T * g : T * (g + 1)].bitcast(FP8X4), rhs_scale=hs[:, T * g : T * (g + 1)],
+                    start=(g == 0), stop=(g == 3),
+                )
+
+        def passes(b, tp, ct):
+            hq, hs = state[("hq", b, tp)]
+            for g in range(4):
+                cols = slice(C * g + P * ct, C * g + P * (ct + 1))
+                nc.tensor.matmul_mx(
+                    out=accumulator(b, ct)[:, 256 * tp : 256 * (tp + 1)],
+                    lhsT=wq[:, cols].bitcast(FP8X4), lhsT_scale=ws[:, cols],
+                    rhs=hq[:, 256 * g : 256 * (g + 1)].bitcast(FP8X4), rhs_scale=hs[:, 256 * g : 256 * (g + 1)],
+                    start=(g == 0), stop=(g == 3),
+                )
+
+        def all_passes(b, tp):
+            for ct in range(4):
+                passes(b, tp, ct)
 
         def sigmoid(b, ct, lo=0, hi=T):
             if lo == 0:
@@ -228,7 +244,9 @@ def tile_dynamicmemorybank_pb_kernel(tc, h, x, memory, w2, b2, out):
                 state[("pm", j)] = pm
 
         def memory_evac(j):
-            nc.scalar.mul(out=memq[:, 1024 * j : 1024 * (j + 1)], in_=state[("pm", j)][:], mul=-0.25)
+            nc.vector.tensor_scalar(
+                out=memq[:, 1024 * j : 1024 * (j + 1)], in0=state[("pm", j)][:], scalar1=-0.25, scalar2=None, op0=ALU.mult
+            )
 
         def x_sums(i):
             px = ps_tp.tile([P, 8 * NX], F32, name="px", tag="tp")
@@ -278,7 +296,7 @@ def tile_dynamicmemorybank_pb_kernel(tc, h, x, memory, w2, b2, out):
                 )
 
         def store(ct, eng, t0=0, t1=4):
-            ot = work.tile([P, P * (t1 - t0)], F32, name="ot", tag="ot", bufs=5)
+            ot = work.tile([P, P * (t1 - t0)], F32, name="ot", tag="ot", bufs=4)
             if eng == "S":
                 nc.scalar.copy(out=ot[:], in_=state[("pf", ct, t0)][:])
             else:
@@ -294,54 +312,57 @@ def tile_dynamicmemorybank_pb_kernel(tc, h, x, memory, w2, b2, out):
             )
 
         keep_clock(5)
-        transposes(0); evacs(0, "S", "S"); regroup_w(0)
-        quant_h(0); quant_w(0)
-        keep_clock(3)
-        transposes(1); evacs(1, "S", "V"); regroup_w(1); quant_h(1); quant_w(1)
-        passes(0)
-        transposes(2); evacs(2, "S", "V"); regroup_w(2); quant_h(2); quant_w(2)
-        passes(1)
-        transposes(3); evacs(3, "S", "V"); regroup_w(3); split_words(4); quant_h(3); split_words(5); quant_w(3)
-        passes(2)
+        transposes(0, 0, True)
+        evac(0, 0, 0, "V"); evac(0, 0, 1, "S"); evac(0, 0, 2, "S"); evac(0, 0, 3, "V")
+        transposes(0, 1, True)
+        for g in range(4):
+            quant_first(0, g)
+        evac(0, 1, 0, "S"); regroup_w(0); evac(0, 1, 1, "S")
+        keep_clock(2)
+        quant_first(1, 0); quant_w(0); regroup_w(1)
+        evac(0, 1, 2, "S"); evac(0, 1, 3, "S")
+        first_passes(0)
+        quant_first(1, 1); quant_w(1); quant_first(1, 2); quant_first(1, 3)
+        first_passes(1)
+        split_words(1, 0, "S"); split_words(1, 1)
+        regroup_w(2); quant_w(2); regroup_w(3)
+        transposes(1, 0)
+        quant_w(3)
+        evac(1, 0, 0, "S"); evac(1, 0, 1, "S"); evac(1, 0, 2, "S"); evac(1, 0, 3, "S")
+        split_words(1, 2); split_words(1, 3)
         bias_transpose()
-        transposes(4); transposes(5); evacs(4, "S", "S"); evacs(5, "S", "S")
-        split_words(6); quant_h(4); split_words(7); quant_h(5)
-        passes(3); sigmoids(0)
-        transposes(6); transposes(7); evacs(6, "V", "S"); evacs(7, "V", "S")
-        passes(4); passes(5)
-        quant_h(6); split_words(8); quant_h(7); split_words(9)
+        first_passes(2); first_passes(3); sigmoids(0)
+        quant(1, 0, 0); quant(1, 0, 1)
         memory_transposes(); memory_evac(0); memory_evac(1)
+        transposes(1, 1); evacs(1, 1, "SSVV")
+        split_words(2, 0); quant(1, 1, 0); split_words(2, 1); quant(1, 1, 1)
+        all_passes(1, 0)
         x_sums(0)
-        transposes(8); transposes(9); evacs(8, "S", "S"); evacs(9, "S", "S")
-        split_words(10); blend(0, 0); split_words(11); quant_h(8); blend(0, 1); quant_h(9); blend(0, 2)
-        passes(6); passes(7); sigmoids(1)
-        transposes(10); transposes(11); evacs(10, "S", "S"); evacs(11, "S", "S")
-        split_words(12); blend(0, 3); split_words(13); blend(1, 0); quant_h(10); blend(1, 1); quant_h(11)
-        passes(8); passes(9)
+        transposes(2, 0); evacs(2, 0, "SSSS")
+        blend(0, 0); split_words(2, 2); blend(0, 1); split_words(2, 3); quant(2, 0, 0); blend(0, 2); quant(2, 0, 1); blend(0, 3)
+        for ct in range(4):
+            passes(1, 1, ct); sigmoid(1, ct)
+        transposes(2, 1); evacs(2, 1, "SSSS"); split_words(3, 0, "S")
+        add_memory(0); split_words(3, 1); add_memory(1); quant(2, 1, 0); blend(1, 0); quant(2, 1, 1); blend(1, 1)
+        all_passes(2, 0)
         x_sums(1)
-        transposes(12); transposes(13); evacs(12, "S", "S"); evacs(13, "S", "S")
-        split_words(14); split_words(15); add_memory(0); quant_h(12); add_memory(1); quant_h(13); blend(1, 2); blend(1, 3)
-        passes(10); passes(11); sigmoids(2)
-        transposes(14); transposes(15); evacs(14, "V", "S"); evacs(15, "S", "S")
-        blend(2, 0); blend(2, 1); quant_h(14); blend(2, 2); quant_h(15)
-        passes(12); passes(13)
-        blend(2, 3); add_up(1, 3); add_up(2, 3)
-        for ct in range(3):
-            mx_pass(14, ct)
-            mx_pass(15, ct)
-            sigmoid(3, ct)
-        mx_pass(14, 3); mx_pass(15, 3); sigmoid(3, 3, 0, 256); sigmoid(3, 3, 256, 512)
-        for b in range(3):
-            sum_part(0, b, b == 0, False)
-        for b in range(3):
-            sum_part(1, b, b == 0, False)
-        blend(3, 0); sum_part(0, 3, False, True); store(0, "S")
-        for b in range(3):
-            sum_part(2, b, b == 0, False)
-        blend(3, 1); sum_part(1, 3, False, True); store(1, "S")
-        sum_part(3, 0, True, False, 0, 2)
-        blend(3, 2); sum_part(2, 3, False, True)
-        blend(3, 3, 0, 256); blend(3, 3, 256, 512); store(2, "V")
-        sum_part(3, 3, False, True, 0, 2); store(3, "V", 0, 2)
-        sum_part(3, 0, True, False, 2, 4)
-        sum_part(3, 3, False, True, 2, 4); store(3, "V", 2, 4)
+        transposes(3, 0); evacs(3, 0, "SSSS")
+        blend(1, 2); split_words(3, 2); quant(3, 0, 0); split_words(3, 3); quant(3, 0, 1)
+        for ct in range(4):
+            passes(2, 1, ct); sigmoid(2, ct)
+        blend(1, 3); add_up(1, 0); add_up(1, 1)
+        transposes(3, 1); evacs(3, 1, "VSVS")
+        quant(3, 1, 0); blend(2, 0); quant(3, 1, 1)
+        all_passes(3, 0)
+        sum_part(0, 0, True, False); sum_part(1, 0, True, False)
+        for ct in range(4):
+            passes(3, 1, ct); sigmoid(3, ct)
+        blend(2, 1); blend(2, 2); blend(2, 3); add_up(1, 2); add_up(1, 3)
+        sum_part(0, 2, False, False); sum_part(1, 2, False, False)
+        sum_part(2, 2, True, False); sum_part(3, 2, True, False)
+        sum_part(2, 0, False, False); sum_part(3, 0, False, False)
+        for ct in range(4):
+            blend(3, ct)
+        for ct in range(4):
+            sum_part(ct, 3, False, True)
+            store(ct, "SSVV"[ct])

@@ -60,20 +60,28 @@ def tile_dynamicmemorybank_pb_kernel(tc, h, x, memory, w2, b2, out):
                 out=w_raw[g][:], in_=w2[512 * g : 512 * (g + 1), :].rearrange("(p j) c -> p (j c)", j=4)
             )
 
-        def load_h(b, t0, t1):
-            ht = keep.tile([P, (t1 - t0) * F], BF16, name="h_%d_%d" % (b, t0))
+        def load_h(b, t0, t1, g0=0, g1=4):
+            n = 512 * (g1 - g0)
+            ht = keep.tile([P, (t1 - t0) * n], BF16, name="h_%d_%d_%d" % (b, t0, g0))
             nc.sync.dma_start(
-                out=ht[:].rearrange("p (t k) -> p t k", t=t1 - t0), in_=h[b].rearrange("(p t) k -> p t k", t=4)[:, t0:t1, :]
+                out=ht[:].rearrange("p (t k) -> p t k", t=t1 - t0),
+                in_=h[b].rearrange("(p t) k -> p t k", t=4)[:, t0:t1, 512 * g0 : 512 * g1],
             )
             for t in range(t0, t1):
-                pieces[(b, t)] = ht[:].bitcast(F32)[:, (F // 2) * (t - t0) : (F // 2) * (t - t0 + 1)]
+                for g in range(g0, g1):
+                    w0 = (n * (t - t0) + 512 * (g - g0)) // 2
+                    pieces[(b, t, g)] = ht[:].bitcast(F32)[:, w0 : w0 + 256]
+                if g1 - g0 == 4:
+                    pieces[(b, t)] = ht[:].bitcast(F32)[:, 1024 * (t - t0) : 1024 * (t - t0 + 1)]
 
         def load_x(b):
             nc.sync.dma_start(out=x_sb[b][:], in_=x[b].rearrange("(p j) c -> p (j c)", j=4))
 
-        for t in range(4):
-            load_h(0, t, t + 1)
+        for g in range(4):
+            load_h(0, 0, 2, g, g + 1)
         load_w(0)
+        load_h(0, 2, 4, 0, 2)
+        load_h(0, 2, 4, 2, 4)
         load_w(1)
         load_h(1, 0, 1)
         load_h(1, 1, 2)
@@ -81,9 +89,9 @@ def tile_dynamicmemorybank_pb_kernel(tc, h, x, memory, w2, b2, out):
         load_w(3)
         load_h(1, 2, 4)
         nc.sync.dma_start(out=mem_sb[:], in_=memory[0].rearrange("(p t) c -> p (t c)", t=4))
-        load_h(2, 0, 2)
         load_x(0)
         load_x(1)
+        load_h(2, 0, 2)
         load_h(2, 2, 4)
         load_h(3, 0, 2)
         load_x(2)
@@ -138,18 +146,18 @@ def tile_dynamicmemorybank_pb_kernel(tc, h, x, memory, w2, b2, out):
                 pieces[(b, t)].rearrange("p (g w u) -> p g u w", g=4, u=2),
             )
 
-        def transposes(b, tp, by_token=False):
-            xt = [ps_tp.tile([P, 512], F32, name="xt", tag="tp") for g in range(4)]
-            state[("xt", b, tp)] = xt
-            runs = [(g, tl) for tl in range(2) for g in range(4)] if by_token else [(g, tl) for g in range(4) for tl in range(2)]
-            for g, tl in runs:
-                for u in range(2):
-                    t = 2 * tp + tl
-                    if ("hp", b, t) in state:
-                        src = state[("hp", b, t)][:, 256 * g + P * u : 256 * g + P * (u + 1)]
-                    else:
-                        src = pieces[(b, t)][:, 256 * g + u : 256 * (g + 1) + u - 1 : 2]
-                    nc.tensor.transpose(out=xt[g][:, 256 * u + P * tl : 256 * u + P * (tl + 1)], in_=src, identity=ident32[:])
+        def transposes(b, tp, groups=(0, 1, 2, 3)):
+            for g in groups:
+                xt = ps_tp.tile([P, 512], F32, name="xt", tag="tp")
+                state[("xt", b, tp, g)] = xt
+                for tl in range(2):
+                    for u in range(2):
+                        t = 2 * tp + tl
+                        if ("hp", b, t) in state:
+                            src = state[("hp", b, t)][:, 256 * g + P * u : 256 * g + P * (u + 1)]
+                        else:
+                            src = pieces[(b, t, g)][:, u : 255 + u : 2]
+                        nc.tensor.transpose(out=xt[:, 256 * u + P * tl : 256 * u + P * (tl + 1)], in_=src, identity=ident32[:])
 
         def evac(b, tp, g, eng):
             if g == 0:
@@ -158,7 +166,7 @@ def tile_dynamicmemorybank_pb_kernel(tc, h, x, memory, w2, b2, out):
             copy_on(
                 eng,
                 gh[:].bitcast(F32)[:, 512 * g : 512 * (g + 1)].rearrange("p (n u) -> p n u", u=2),
-                state[("xt", b, tp)][g][:].rearrange("p (u n) -> p n u", u=2),
+                state[("xt", b, tp, g)][:].rearrange("p (u n) -> p n u", u=2),
             )
 
         def evacs(b, tp, engs):
@@ -312,57 +320,60 @@ def tile_dynamicmemorybank_pb_kernel(tc, h, x, memory, w2, b2, out):
             )
 
         keep_clock(5)
-        transposes(0, 0, True)
-        evac(0, 0, 0, "V"); evac(0, 0, 1, "S"); evac(0, 0, 2, "S"); evac(0, 0, 3, "V")
-        transposes(0, 1, True)
+        transposes(0, 0)
+        evac(0, 0, 0, "S"); evac(0, 0, 1, "V"); evac(0, 0, 2, "S"); evac(0, 0, 3, "V")
         for g in range(4):
             quant_first(0, g)
-        evac(0, 1, 0, "S"); regroup_w(0); evac(0, 1, 1, "S")
         keep_clock(2)
-        quant_first(1, 0); quant_w(0); regroup_w(1)
-        evac(0, 1, 2, "S"); evac(0, 1, 3, "S")
+        bias_transpose()
+        regroup_w(0); quant_w(0)
+        transposes(0, 1)
+        evac(0, 1, 0, "S"); quant_first(1, 0); evac(0, 1, 1, "S"); quant_first(1, 1)
+        evac(0, 1, 2, "S"); regroup_w(1); evac(0, 1, 3, "S")
+        quant_first(1, 2); quant_w(1); quant_first(1, 3)
         first_passes(0)
-        quant_first(1, 1); quant_w(1); quant_first(1, 2); quant_first(1, 3)
         first_passes(1)
         split_words(1, 0, "S"); split_words(1, 1)
         regroup_w(2); quant_w(2); regroup_w(3)
         transposes(1, 0)
-        quant_w(3)
-        evac(1, 0, 0, "S"); evac(1, 0, 1, "S"); evac(1, 0, 2, "S"); evac(1, 0, 3, "S")
-        split_words(1, 2); split_words(1, 3)
-        bias_transpose()
+        evac(1, 0, 0, "S"); evac(1, 0, 1, "S"); quant_w(3)
+        evac(1, 0, 2, "S"); evac(1, 0, 3, "S")
+        split_words(1, 2); quant(1, 0, 0); split_words(1, 3)
         first_passes(2); first_passes(3); sigmoids(0)
-        quant(1, 0, 0); quant(1, 0, 1)
+        quant(1, 0, 1)
         memory_transposes(); memory_evac(0); memory_evac(1)
         transposes(1, 1); evacs(1, 1, "SSVV")
-        split_words(2, 0); quant(1, 1, 0); split_words(2, 1); quant(1, 1, 1)
-        all_passes(1, 0)
         x_sums(0)
+        quant(1, 1, 0)
+        all_passes(1, 0)
+        blend(0, 0); quant(1, 1, 1); split_words(2, 0, "S"); split_words(2, 1, "S"); blend(0, 1)
         transposes(2, 0); evacs(2, 0, "SSSS")
-        blend(0, 0); split_words(2, 2); blend(0, 1); split_words(2, 3); quant(2, 0, 0); blend(0, 2); quant(2, 0, 1); blend(0, 3)
+        blend(0, 2); blend(0, 3); split_words(2, 2); quant(2, 0, 0); split_words(2, 3); quant(2, 0, 1)
         for ct in range(4):
             passes(1, 1, ct); sigmoid(1, ct)
-        transposes(2, 1); evacs(2, 1, "SSSS"); split_words(3, 0, "S")
-        add_memory(0); split_words(3, 1); add_memory(1); quant(2, 1, 0); blend(1, 0); quant(2, 1, 1); blend(1, 1)
+        add_memory(0); add_memory(1)
+        transposes(2, 1); evacs(2, 1, "SSSS")
+        split_words(3, 0); blend(1, 0); split_words(3, 1); blend(1, 1); quant(2, 1, 0); blend(1, 2); quant(2, 1, 1); blend(1, 3)
         all_passes(2, 0)
         x_sums(1)
         transposes(3, 0); evacs(3, 0, "SSSS")
-        blend(1, 2); split_words(3, 2); quant(3, 0, 0); split_words(3, 3); quant(3, 0, 1)
+        add_up(1, 0); add_up(1, 1); split_words(3, 2); quant(3, 0, 0); split_words(3, 3); quant(3, 0, 1)
         for ct in range(4):
             passes(2, 1, ct); sigmoid(2, ct)
-        blend(1, 3); add_up(1, 0); add_up(1, 1)
-        transposes(3, 1); evacs(3, 1, "VSVS")
-        quant(3, 1, 0); blend(2, 0); quant(3, 1, 1)
+        add_up(1, 2); add_up(1, 3)
+        transposes(3, 1); evacs(3, 1, "SSSS")
+        blend(2, 0); blend(2, 1); quant(3, 1, 0); blend(2, 2); quant(3, 1, 1); blend(2, 3)
         all_passes(3, 0)
         sum_part(0, 0, True, False); sum_part(1, 0, True, False)
         for ct in range(4):
             passes(3, 1, ct); sigmoid(3, ct)
-        blend(2, 1); blend(2, 2); blend(2, 3); add_up(1, 2); add_up(1, 3)
+        add_up(2, 2); add_up(2, 3)
         sum_part(0, 2, False, False); sum_part(1, 2, False, False)
-        sum_part(2, 2, True, False); sum_part(3, 2, True, False)
-        sum_part(2, 0, False, False); sum_part(3, 0, False, False)
-        for ct in range(4):
-            blend(3, ct)
-        for ct in range(4):
-            sum_part(ct, 3, False, True)
-            store(ct, "SSVV"[ct])
+        blend(3, 0); sum_part(0, 3, False, True); store(0, "S")
+        sum_part(2, 0, True, False)
+        blend(3, 1); sum_part(1, 3, False, True); store(1, "S")
+        sum_part(3, 0, True, False)
+        blend(3, 2); sum_part(2, 3, False, True)
+        blend(3, 3); sum_part(3, 3, False, True)
+        store(2, "V")
+        store(3, "V")

@@ -38,16 +38,16 @@ def tile_dynamicmemorybank_pb_kernel(tc, h, x, memory, w2, b2, out):
         identb = const.tile([P, P], BF16, name="identb")
         ones = const.tile([P, NX], BF16, name="ones")
         b2rows = const.tile([P, P], BF16, name="b2rows")
-        b2col = const.tile([P, 4], F32, name="b2col")
+        b2neg = const.tile([P, 4], F32, name="b2neg")
         warm = const.tile([P, 2], F32, name="warm")
-        idle = const.tile([P, T], BF16, name="idle")
-        nc.vector.memset(idle[:], 0.0)
+        idle = const.tile([P, 256], BF16, name="idle")
         make_identity(nc, ident32[:])
         make_identity(nc, identb[:])
         nc.vector.memset(b2rows[:], 0.0)
-        nc.vector.memset(ones[:], 1.0)
         nc.vector.memset(warm[:], 0.0)
-        nc.scalar.dma_start(out=b2rows[0:4, :], in_=b2.rearrange("(r c) -> r c", r=4))
+        nc.vector.memset(idle[:], 0.0)
+        nc.vector.memset(ones[:], 1.0)
+        nc.sync.dma_start(out=b2rows[0:4, :], in_=b2.rearrange("(r c) -> r c", r=4))
         nc.scalar.activation(out=warm[:, 1:2], in_=warm[:, 0:1], func=ACT.Sigmoid)
 
         w_raw = [keep.tile([P, 4 * C], BF16, name="w_raw%d" % g) for g in range(4)]
@@ -101,7 +101,8 @@ def tile_dynamicmemorybank_pb_kernel(tc, h, x, memory, w2, b2, out):
         wq = keep.tile([P, 4 * C], U32, name="wq", align_bytes=64)
         ws = keep.tile([P, 4 * C], U8, name="ws", align_bytes=64)
         memq = keep.tile([P, 4 * T], BF16, name="memq")
-        xm4 = [keep.tile([P, 8], F32, name="xm4_%d" % i) for i in range(2)]
+        xm4 = keep.tile([P, 16], F32, name="xm4")
+        xbar = keep.tile([P, 4], F32, name="xbar")
 
         state = {}
 
@@ -130,12 +131,12 @@ def tile_dynamicmemorybank_pb_kernel(tc, h, x, memory, w2, b2, out):
         def keep_clock(n):
             pw = ps_acc.tile([P, T], F32, name="pw", tag="acc")
             for i in range(n):
-                nc.tensor.matmul(out=pw[:], lhsT=idle[:, 0:P], rhs=idle[:], start=True, stop=True)
+                nc.tensor.matmul(out=pw[:, 0:256], lhsT=idle[:, 0:P], rhs=idle[:], start=True, stop=True)
 
         def bias_transpose():
             pb = ps_tp.tile([P, P], BF16, name="pb", tag="tp")
             nc.tensor.transpose(out=pb[:], in_=b2rows[:], identity=identb[:])
-            nc.scalar.copy(out=b2col[:], in_=pb[:, 0:4])
+            nc.scalar.mul(out=b2neg[:], in_=pb[:, 0:4], mul=-1.0)
 
         def split_words(b, t, eng="V"):
             hp = work.tile([P, F // 2], F32, name="hp", tag="hp", bufs=4)
@@ -232,7 +233,7 @@ def tile_dynamicmemorybank_pb_kernel(tc, h, x, memory, w2, b2, out):
                 state[("gt", b, ct)] = keep.tile([P, T], F32, name="gt_%d_%d" % (b, ct))
             nc.scalar.activation(
                 out=state[("gt", b, ct)][:, lo:hi], in_=state[("acc", b, ct)][:, lo:hi], func=ACT.Sigmoid,
-                bias=b2col[:, ct : ct + 1], scale=1.0,
+                bias=b2neg[:, ct : ct + 1], scale=-1.0,
             )
 
         def sigmoids(b):
@@ -253,7 +254,7 @@ def tile_dynamicmemorybank_pb_kernel(tc, h, x, memory, w2, b2, out):
 
         def memory_evac(j):
             nc.vector.tensor_scalar(
-                out=memq[:, 1024 * j : 1024 * (j + 1)], in0=state[("pm", j)][:], scalar1=-0.25, scalar2=None, op0=ALU.mult
+                out=memq[:, 1024 * j : 1024 * (j + 1)], in0=state[("pm", j)][:], scalar1=0.25, scalar2=None, op0=ALU.mult
             )
 
         def x_sums(i):
@@ -269,7 +270,7 @@ def tile_dynamicmemorybank_pb_kernel(tc, h, x, memory, w2, b2, out):
                             stop=(j == 3),
                         )
             nc.scalar.mul(
-                out=xm4[i][:].rearrange("p (c o) -> p c o", o=1),
+                out=xm4[:, 8 * i : 8 * (i + 1)].rearrange("p (c o) -> p c o", o=1),
                 in_=px[:].rearrange("p (c n) -> p c n", n=NX)[:, :, 0:1],
                 mul=1.0 / (4 * T),
             )
@@ -278,53 +279,53 @@ def tile_dynamicmemorybank_pb_kernel(tc, h, x, memory, w2, b2, out):
             gt = state[("gt", b, ct)]
             nc.vector.scalar_tensor_tensor(
                 out=gt[:, lo:hi], in0=memq[:, T * ct + lo : T * ct + hi],
-                scalar=xm4[b // 2][:, 4 * (b % 2) + ct : 4 * (b % 2) + ct + 1], in1=gt[:, lo:hi],
-                op0=ALU.add, op1=ALU.mult,
+                scalar=xm4[:, 4 * b + ct : 4 * b + ct + 1], in1=gt[:, lo:hi],
+                op0=ALU.subtract, op1=ALU.mult,
+            )
+
+        def x_total():
+            nc.vector.tensor_reduce(
+                out=xbar[:], in_=xm4[:].rearrange("p (b c) -> p c b", c=4), axis=mybir.AxisListType.X, op=ALU.add
+            )
+
+        def add_last(b, ct):
+            t0, t1 = state[("gt", 0, ct)], state[("gt", b, ct)]
+            nc.vector.scalar_tensor_tensor(
+                out=t0[:], in0=t1[:], scalar=xbar[:, ct : ct + 1], in1=t0[:], op0=ALU.add, op1=ALU.add
             )
 
         def add_up(b, ct):
             t0, t1 = state[("gt", 0, ct)], state[("gt", b, ct)]
             nc.vector.tensor_tensor(out=t0[:], in0=t0[:], in1=t1[:], op=ALU.add)
 
-        def add_memory(ct):
-            gt = state[("gt", 0, ct)]
-            nc.vector.scalar_tensor_tensor(
-                out=gt[:], in0=memq[:, T * ct : T * (ct + 1)], scalar=-4.0, in1=gt[:], op0=ALU.mult, op1=ALU.add
-            )
-
-        def sum_part(ct, b, first, last, t0=0, t1=4):
-            if first:
-                state[("pf", ct, t0)] = ps_tp.tile([P, P * (t1 - t0)], F32, name="pf", tag="tp")
-            pf = state[("pf", ct, t0)]
+        def sum_part(b, half, ct):
+            key = ("pf", half, ct // 2)
+            if b == 0 and ct % 2 == 0:
+                state[key] = ps_tp.tile([P, 512], F32, name="pf", tag="tp")
+            pf = state[key]
             src = state[("gt", b, ct)]
-            for tt in range(t0, t1):
+            for tl in range(2):
+                n = 2 * half + tl
+                col = 256 * tl + P * (ct % 2)
                 nc.tensor.matmul(
-                    out=pf[:, P * (tt - t0) : P * (tt - t0 + 1)], lhsT=src[:, P * tt : P * (tt + 1)], rhs=ident32[:],
-                    is_transpose=True, start=(first and tt == t0), stop=(last and tt == t1 - 1),
+                    out=pf[:, col : col + P], lhsT=src[:, P * n : P * (n + 1)], rhs=ident32[:], is_transpose=True,
+                    start=(b == 0 and ct % 2 == 0 and tl == 0), stop=(b == 3 and ct % 2 == 1 and tl == 1),
                 )
 
-        def store(ct, eng, t0=0, t1=4):
-            ot = work.tile([P, P * (t1 - t0)], F32, name="ot", tag="ot", bufs=4)
-            if eng == "S":
-                nc.scalar.copy(out=ot[:], in_=state[("pf", ct, t0)][:])
-            else:
-                nc.vector.tensor_tensor(
-                    out=ot[:].rearrange("p (t c) -> p t c", t=t1 - t0),
-                    in0=state[("pf", ct, t0)][:].rearrange("p (t c) -> p t c", t=t1 - t0),
-                    in1=mem_sb[:].rearrange("p (t c) -> p t c", t=4)[:, t0:t1, P * ct : P * (ct + 1)],
-                    op=ALU.add,
-                )
+        def store(half, pair, eng):
+            ot = work.tile([P, 512], F32, name="ot", tag="ot", bufs=4)
+            copy_on(eng, ot[:], state[("pf", half, pair)][:])
             nc.sync.dma_start(
-                out=out[0].rearrange("(p t) c -> p t c", t=4)[:, t0:t1, P * ct : P * (ct + 1)],
-                in_=ot[:].rearrange("p (t c) -> p t c", t=t1 - t0),
+                out=out[0].rearrange("(p t) c -> p t c", t=4)[:, 2 * half : 2 * half + 2, 256 * pair : 256 * (pair + 1)],
+                in_=ot[:].rearrange("p (t c) -> p t c", t=2),
             )
 
-        keep_clock(5)
+        keep_clock(8)
         transposes(0, 0)
         evac(0, 0, 0, "S"); evac(0, 0, 1, "V"); evac(0, 0, 2, "S"); evac(0, 0, 3, "V")
         for g in range(4):
             quant_first(0, g)
-        keep_clock(2)
+        keep_clock(4)
         bias_transpose()
         regroup_w(0); quant_w(0)
         transposes(0, 1)
@@ -351,29 +352,32 @@ def tile_dynamicmemorybank_pb_kernel(tc, h, x, memory, w2, b2, out):
         blend(0, 2); blend(0, 3); split_words(2, 2); quant(2, 0, 0); split_words(2, 3); quant(2, 0, 1)
         for ct in range(4):
             passes(1, 1, ct); sigmoid(1, ct)
-        add_memory(0); add_memory(1)
         transposes(2, 1); evacs(2, 1, "SSSS")
-        split_words(3, 0); blend(1, 0); split_words(3, 1); blend(1, 1); quant(2, 1, 0); blend(1, 2); quant(2, 1, 1); blend(1, 3)
+        split_words(3, 0); blend(1, 0); split_words(3, 1); blend(1, 1); add_up(1, 0); quant(2, 1, 0); blend(1, 2); quant(2, 1, 1); blend(1, 3)
         all_passes(2, 0)
+        split_words(3, 2, "S")
         x_sums(1)
         transposes(3, 0); evacs(3, 0, "SSSS")
-        add_up(1, 0); add_up(1, 1); split_words(3, 2); quant(3, 0, 0); split_words(3, 3); quant(3, 0, 1)
+        x_total(); add_up(1, 1); add_up(1, 2); quant(3, 0, 0); split_words(3, 3); quant(3, 0, 1)
         for ct in range(4):
             passes(2, 1, ct); sigmoid(2, ct)
-        add_up(1, 2); add_up(1, 3)
+        add_up(1, 3)
         transposes(3, 1); evacs(3, 1, "SSSS")
-        blend(2, 0); blend(2, 1); quant(3, 1, 0); blend(2, 2); quant(3, 1, 1); blend(2, 3)
+        blend(2, 0); blend(2, 1); add_last(2, 0); add_last(2, 1); quant(3, 1, 0); blend(2, 2); quant(3, 1, 1); blend(2, 3)
         all_passes(3, 0)
-        sum_part(0, 0, True, False); sum_part(1, 0, True, False)
         for ct in range(4):
-            passes(3, 1, ct); sigmoid(3, ct)
-        add_up(2, 2); add_up(2, 3)
-        sum_part(0, 2, False, False); sum_part(1, 2, False, False)
-        blend(3, 0); sum_part(0, 3, False, True); store(0, "S")
-        sum_part(2, 0, True, False)
-        blend(3, 1); sum_part(1, 3, False, True); store(1, "S")
-        sum_part(3, 0, True, False)
-        blend(3, 2); sum_part(2, 3, False, True)
-        blend(3, 3); sum_part(3, 3, False, True)
-        store(2, "V")
-        store(3, "V")
+            sigmoid(3, ct, 0, 256)
+        sum_part(0, 0, 0); sum_part(0, 0, 1)
+        for ct in range(4):
+            passes(3, 1, ct); sigmoid(3, ct, 256, 512)
+        add_last(2, 2); add_last(2, 3)
+        for ct in range(4):
+            blend(3, ct, 0, 256)
+        sum_part(0, 0, 2); sum_part(0, 0, 3); sum_part(0, 1, 0); sum_part(0, 1, 1)
+        sum_part(3, 0, 0); sum_part(3, 0, 1); store(0, 0, "S")
+        sum_part(0, 1, 2); sum_part(0, 1, 3)
+        sum_part(3, 0, 2); sum_part(3, 0, 3); store(0, 1, "S")
+        for ct in range(4):
+            blend(3, ct, 256, 512)
+        sum_part(3, 1, 0); sum_part(3, 1, 1); store(1, 0, "S")
+        sum_part(3, 1, 2); sum_part(3, 1, 3); store(1, 1, "V")

@@ -65,7 +65,7 @@ def tile_dynamicmemorybank_pb_kernel(tc, h, x, memory, w2, b2, out):
             ht = keep.tile([P, (t1 - t0) * n], BF16, name="h_%d_%d_%d" % (b, t0, g0))
             nc.sync.dma_start(
                 out=ht[:].rearrange("p (t k) -> p t k", t=t1 - t0),
-                in_=h[b].rearrange("(p t) k -> p t k", t=4)[:, t0:t1, 512 * g0 : 512 * g1],
+                in_=h[b].rearrange("(t p) k -> p t k", t=4)[:, t0:t1, 512 * g0 : 512 * g1],
             )
             for t in range(t0, t1):
                 for g in range(g0, g1):
@@ -88,7 +88,9 @@ def tile_dynamicmemorybank_pb_kernel(tc, h, x, memory, w2, b2, out):
         load_w(2)
         load_w(3)
         load_h(1, 2, 4)
-        nc.sync.dma_start(out=mem_sb[:], in_=memory[0].rearrange("(p t) c -> p (t c)", t=4))
+        nc.sync.dma_start(
+            out=mem_sb[:].rearrange("p (t c) -> p t c", t=4), in_=memory[0].rearrange("(t p) c -> p t c", t=4)
+        )
         load_x(0)
         load_x(1)
         load_h(2, 0, 2)
@@ -316,7 +318,7 @@ def tile_dynamicmemorybank_pb_kernel(tc, h, x, memory, w2, b2, out):
             ot = work.tile([P, 512], F32, name="ot", tag="ot", bufs=4)
             copy_on(eng, ot[:], state[("pf", half, pair)][:])
             nc.sync.dma_start(
-                out=out[0].rearrange("(p t) c -> p t c", t=4)[:, 2 * half : 2 * half + 2, 256 * pair : 256 * (pair + 1)],
+                out=out[0].rearrange("(t p) c -> p t c", t=4)[:, 2 * half : 2 * half + 2, 256 * pair : 256 * (pair + 1)],
                 in_=ot[:].rearrange("p (t c) -> p t c", t=2),
             )
 

@@ -47,7 +47,6 @@ def tile_dynamicmemorybank_pb_kernel(tc, h, x, memory, w2, b2, out):
         nc.vector.memset(warm[:], 0.0)
         nc.vector.memset(idle[:], 0.0)
         nc.vector.memset(ones[:], 1.0)
-        nc.sync.dma_start(out=b2rows[0:4, :], in_=b2.rearrange("(r c) -> r c", r=4))
         nc.scalar.activation(out=warm[:, 1:2], in_=warm[:, 0:1], func=ACT.Sigmoid)
 
         w_raw = [keep.tile([P, 4 * C], BF16, name="w_raw%d" % g) for g in range(4)]
@@ -77,8 +76,11 @@ def tile_dynamicmemorybank_pb_kernel(tc, h, x, memory, w2, b2, out):
         def load_x(b):
             nc.sync.dma_start(out=x_sb[b][:], in_=x[b].rearrange("(p j) c -> p (j c)", j=4))
 
-        for g in range(4):
+        load_h(0, 0, 1, 0, 1)
+        load_h(0, 1, 2, 0, 1)
+        for g in range(1, 4):
             load_h(0, 0, 2, g, g + 1)
+        nc.sync.dma_start(out=b2rows[0:4, :], in_=b2.rearrange("(r c) -> r c", r=4))
         load_w(0)
         load_h(0, 2, 4, 0, 2)
         load_h(0, 2, 4, 2, 4)
@@ -324,7 +326,7 @@ def tile_dynamicmemorybank_pb_kernel(tc, h, x, memory, w2, b2, out):
 
         keep_clock(8)
         transposes(0, 0)
-        evac(0, 0, 0, "S"); evac(0, 0, 1, "V"); evac(0, 0, 2, "S"); evac(0, 0, 3, "V")
+        evacs(0, 0, "SSSS")
         for g in range(4):
             quant_first(0, g)
         keep_clock(4)
@@ -349,7 +351,7 @@ def tile_dynamicmemorybank_pb_kernel(tc, h, x, memory, w2, b2, out):
         x_sums(0)
         quant(1, 1, 0)
         all_passes(1, 0)
-        blend(0, 0); quant(1, 1, 1); split_words(2, 0, "S"); split_words(2, 1, "S"); blend(0, 1)
+        quant(1, 1, 1); split_words(2, 0, "S"); split_words(2, 1); blend(0, 0); blend(0, 1)
         transposes(2, 0); evacs(2, 0, "SSSS")
         blend(0, 2); blend(0, 3); split_words(2, 2); quant(2, 0, 0); split_words(2, 3); quant(2, 0, 1)
         for ct in range(4):

@@ -371,14 +371,14 @@ def tile_dynamicmemorybank_pb_kernel(tc, h, x, memory, w2, b2, out):
         all_passes(3, 0)
         for ct in range(4):
             sigmoid(3, ct, 0, 256)
-        sum_part(0, 0, 0); sum_part(0, 0, 1)
+        sum_part(0, 0, 0); sum_part(0, 0, 1); sum_part(0, 1, 0); sum_part(0, 1, 1)
         for ct in range(4):
             passes(3, 1, ct); sigmoid(3, ct, 256, 512)
+        blend(3, 0, 0, 256); blend(3, 1, 0, 256)
         add_last(2, 2); add_last(2, 3)
-        for ct in range(4):
-            blend(3, ct, 0, 256)
-        sum_part(0, 0, 2); sum_part(0, 0, 3); sum_part(0, 1, 0); sum_part(0, 1, 1)
+        blend(3, 2, 0, 256); blend(3, 3, 0, 256)
         sum_part(3, 0, 0); sum_part(3, 0, 1); store(0, 0, "S")
+        sum_part(0, 0, 2); sum_part(0, 0, 3)
         sum_part(0, 1, 2); sum_part(0, 1, 3)
         sum_part(3, 0, 2); sum_part(3, 0, 3); store(0, 1, "S")
         for ct in range(4):

from contextlib import ExitStack

import concourse.bass as bass
import concourse.mybir as mybir
import concourse.tile as tile
from concourse.masks import make_identity

F32 = mybir.dt.float32
BF16 = mybir.dt.bfloat16
U32 = mybir.dt.uint32
U8 = mybir.dt.uint8
FP8X4 = mybir.dt.float8_e4m3fn_x4
ALU = mybir.AluOpType
ACT = mybir.ActivationFunctionType

P = 128
B = 4
T = 512
C = 512
F = 2048
FLOPS = 2 * B * T * F * C

W_GROUPS_ON_VECTOR = 84
NX = 32


def tile_dynamicmemorybank_pb_kernel(tc, h, x, memory, w2, b2, out):
    nc = tc.nc
    with ExitStack() as ctx:
        const = ctx.enter_context(tc.tile_pool(name="const", bufs=1))
        keep = ctx.enter_context(tc.tile_pool(name="keep", bufs=1))
        work = ctx.enter_context(tc.tile_pool(name="work", bufs=2))
        ps_acc = ctx.enter_context(tc.psum_pool(name="psacc", bufs=4))
        ps_tp = ctx.enter_context(tc.psum_pool(name="pstp", bufs=4))
        ctx.enter_context(tc.manual_schedule())

        ident32 = const.tile([P, P], F32, name="ident32")
        identb = const.tile([P, P], BF16, name="identb")
        ones = const.tile([P, NX], BF16, name="ones")
        b2rows = const.tile([P, P], BF16, name="b2rows")
        b2neg = const.tile([P, 4], F32, name="b2neg")
        warm = const.tile([P, 2], F32, name="warm")
        idle = const.tile([P, 256], BF16, name="idle")
        make_identity(nc, ident32[:])
        make_identity(nc, identb[:])
        nc.vector.memset(b2rows[:], 0.0)
        nc.vector.memset(warm[:], 0.0)
        nc.vector.memset(idle[:], 0.0)
        nc.vector.memset(ones[:], 1.0)
        nc.scalar.activation(out=warm[:, 1:2], in_=warm[:, 0:1], func=ACT.Sigmoid)

        w_raw = [keep.tile([P, 4 * C], BF16, name="w_raw%d" % g) for g in range(4)]
        x_sb = [keep.tile([P, 4 * C], BF16, name="x_sb%d" % b) for b in range(B)]
        mem_sb = keep.tile([P, 4 * C], BF16, name="mem_sb")
        pieces = {}

        def load_w(g):
            nc.sync.dma_start(
                out=w_raw[g][:], in_=w2[512 * g : 512 * (g + 1), :].rearrange("(p j) c -> p (j c)", j=4)
            )

        def load_h(b, t0, t1, g0=0, g1=4):
            n = 512 * (g1 - g0)
            ht = keep.tile([P, (t1 - t0) * n], BF16, name="h_%d_%d_%d" % (b, t0, g0))
            nc.sync.dma_start(
                out=ht[:].rearrange("p (t k) -> p t k", t=t1 - t0),
                in_=h[b].rearrange("(t p) k -> p t k", t=4)[:, t0:t1, 512 * g0 : 512 * g1],
            )
            for t in range(t0, t1):
                for g in range(g0, g1):
                    w0 = (n * (t - t0) + 512 * (g - g0)) // 2
                    pieces[(b, t, g)] = ht[:].bitcast(F32)[:, w0 : w0 + 256]
                if g1 - g0 == 4:
                    pieces[(b, t)] = ht[:].bitcast(F32)[:, 1024 * (t - t0) : 1024 * (t - t0 + 1)]

        def load_x(b):
            nc.sync.dma_start(out=x_sb[b][:], in_=x[b].rearrange("(p j) c -> p (j c)", j=4))

        load_h(0, 0, 1, 0, 1)
        load_h(0, 1, 2, 0, 1)
        for g in range(1, 4):
            load_h(0, 0, 2, g, g + 1)
        nc.sync.dma_start(out=b2rows[0:4, :], in_=b2.rearrange("(r c) -> r c", r=4))
        load_w(0)
        load_h(0, 2, 4, 0, 2)
        load_h(0, 2, 4, 2, 4)
        load_w(1)
        load_h(1, 0, 1)
        load_h(1, 1, 2)
        load_w(2)
        load_w(3)
        load_h(1, 2, 4)
        nc.sync.dma_start(
            out=mem_sb[:].rearrange("p (t c) -> p t c", t=4), in_=memory[0].rearrange("(t p) c -> p t c", t=4)
        )
        load_x(0)
        load_x(1)
        load_h(2, 0, 2)
        load_h(2, 2, 4)
        load_h(3, 0, 2)
        load_x(2)
        load_x(3)
        load_h(3, 2, 4)

        wq = keep.tile([P, 4 * C], U32, name="wq", align_bytes=64)
        ws = keep.tile([P, 4 * C], U8, name="ws", align_bytes=64)
        memq = keep.tile([P, 4 * T], BF16, name="memq")
        xm4 = keep.tile([P, 16], F32, name="xm4")
        xbar = keep.tile([P, 4], F32, name="xbar")

        state = {}

        def copy_on(eng, out_ap, in_ap):
            if eng == "V":
                nc.vector.tensor_copy(out=out_ap, in_=in_ap)
            else:
                nc.scalar.copy(out=out_ap, in_=in_ap)

        def regroup_w(g):
            gw = work.tile([P, 4 * C], BF16, name="gw", tag="gw", bufs=2, align_bytes=64)
            state[("gw", g)] = gw
            dst = gw[:].rearrange("p (c i t) -> p c t i", i=4, t=4)
            src = w_raw[g][:].rearrange("p (t c i) -> p c t i", t=4, i=4)
            n = W_GROUPS_ON_VECTOR
            nc.vector.tensor_copy(out=dst[:, 0:n], in_=src[:, 0:n])
            nc.scalar.copy(out=dst[:, n:128], in_=src[:, n:128])

        def quant_w(g):
            nc.vector.quantize_mx(
                out=wq[:, C * g : C * (g + 1)].bitcast(FP8X4),
                scales=ws[:, C * g : C * (g + 1)],
                in_=state[("gw", g)][:],
            )

        def keep_clock(n):
            pw = ps_acc.tile([P, T], F32, name="pw", tag="acc")
            for i in range(n):
                nc.tensor.matmul(out=pw[:, 0:256], lhsT=idle[:, 0:P], rhs=idle[:], start=True, stop=True)

        def bias_transpose():
            pb = ps_tp.tile([P, P], BF16, name="pb", tag="tp")
            nc.tensor.transpose(out=pb[:], in_=b2rows[:], identity=identb[:])
            nc.scalar.mul(out=b2neg[:], in_=pb[:, 0:4], mul=-1.0)

        def split_words(b, t, eng="V"):
            hp = work.tile([P, F // 2], F32, name="hp", tag="hp", bufs=4)
            state[("hp", b, t)] = hp
            copy_on(
                eng,
                hp[:].rearrange("p (g u w) -> p g u w", g=4, u=2),
                pieces[(b, t)].rearrange("p (g w u) -> p g u w", g=4, u=2),
            )

        def transposes(b, tp, groups=(0, 1, 2, 3)):
            for g in groups:
                xt = ps_tp.tile([P, 512], F32, name="xt", tag="tp")
                state[("xt", b, tp, g)] = xt
                for tl in range(2):
                    for u in range(2):
                        t = 2 * tp + tl
                        if ("hp", b, t) in state:
                            src = state[("hp", b, t)][:, 256 * g + P * u : 256 * g + P * (u + 1)]
                        else:
                            src = pieces[(b, t, g)][:, u : 255 + u : 2]
                        nc.tensor.transpose(out=xt[:, 256 * u + P * tl : 256 * u + P * (tl + 1)], in_=src, identity=ident32[:])

        def evac(b, tp, g, eng):
            if g == 0:
                state[("gh", b, tp)] = work.tile([P, 4096], BF16, name="gh", tag="gh", bufs=3, align_bytes=64)
            gh = state[("gh", b, tp)]
            copy_on(
                eng,
                gh[:].bitcast(F32)[:, 512 * g : 512 * (g + 1)].rearrange("p (n u) -> p n u", u=2),
                state[("xt", b, tp, g)][:].rearrange("p (u n) -> p n u", u=2),
            )

        def evacs(b, tp, engs):
            for g in range(4):
                evac(b, tp, g, engs[g])

        def quant_first(tp, g):
            if tp == 0 and g == 0:
                state[("hq", 0)] = (
                    keep.tile([P, 4 * T], U32, name="hq0", align_bytes=64), keep.tile([P, 4 * T], U8, name="hs0", align_bytes=64)
                )
            hq, hs = state[("hq", 0)]
            c0 = T * g + 256 * tp
            nc.vector.quantize_mx(
                out=hq[:, c0 : c0 + 256].bitcast(FP8X4), scales=hs[:, c0 : c0 + 256],
                in_=state[("gh", 0, tp)][:, 1024 * g : 1024 * (g + 1)],
            )

        def quant(b, tp, gp):
            if gp == 0:
                state[("hq", b, tp)] = (
                    work.tile([P, 1024], U32, name="hq", tag="hq", bufs=3, align_bytes=64),
                    work.tile([P, 1024], U8, name="hs", tag="hs", bufs=3, align_bytes=64),
                )
            hq, hs = state[("hq", b, tp)]
            nc.vector.quantize_mx(
                out=hq[:, 512 * gp : 512 * (gp + 1)].bitcast(FP8X4), scales=hs[:, 512 * gp : 512 * (gp + 1)],
                in_=state[("gh", b, tp)][:, 2048 * gp : 2048 * (gp + 1)],
            )

        def accumulator(b, ct):
            if ("acc", b, ct) not in state:
                state[("acc", b, ct)] = ps_acc.tile([P, T], F32, name="acc", tag="acc")
            return state[("acc", b, ct)]

        def first_passes(g):
            hq, hs = state[("hq", 0)]
            for ct in range(4):
                cols = slice(C * g + P * ct, C * g + P * (ct + 1))
                nc.tensor.matmul_mx(
                    out=accumulator(0, ct)[:], lhsT=wq[:, cols].bitcast(FP8X4), lhsT_scale=ws[:, cols],
                    rhs=hq[:, T * g : T * (g + 1)].bitcast(FP8X4), rhs_scale=hs[:, T * g : T * (g + 1)],
                    start=(g == 0), stop=(g == 3),
                )

        def passes(b, tp, ct):
            hq, hs = state[("hq", b, tp)]
            for g in range(4):
                cols = slice(C * g + P * ct, C * g + P * (ct + 1))
                nc.tensor.matmul_mx(
                    out=accumulator(b, ct)[:, 256 * tp : 256 * (tp + 1)],
                    lhsT=wq[:, cols].bitcast(FP8X4), lhsT_scale=ws[:, cols],
                    rhs=hq[:, 256 * g : 256 * (g + 1)].bitcast(FP8X4), rhs_scale=hs[:, 256 * g : 256 * (g + 1)],
                    start=(g == 0), stop=(g == 3),
                )

        def all_passes(b, tp):
            for ct in range(4):
                passes(b, tp, ct)

        def sigmoid(b, ct, lo=0, hi=T):
            if lo == 0:
                state[("gt", b, ct)] = keep.tile([P, T], F32, name="gt_%d_%d" % (b, ct))
            nc.scalar.activation(
                out=state[("gt", b, ct)][:, lo:hi], in_=state[("acc", b, ct)][:, lo:hi], func=ACT.Sigmoid,
                bias=b2neg[:, ct : ct + 1], scale=-1.0,
            )

        def sigmoids(b):
            for ct in range(4):
                sigmoid(b, ct)

        def memory_transposes():
            for j in range(2):
                pm = ps_tp.tile([P, 1024], BF16, name="pm", tag="tp")
                for cl in range(2):
                    for tt in range(4):
                        nc.tensor.transpose(
                            out=pm[:, 512 * cl + P * tt : 512 * cl + P * (tt + 1)],
                            in_=mem_sb[:, C * tt + P * (2 * j + cl) : C * tt + P * (2 * j + cl + 1)],
                            identity=identb[:],
                        )
                state[("pm", j)] = pm

        def memory_evac(j):
            nc.vector.tensor_scalar(
                out=memq[:, 1024 * j : 1024 * (j + 1)], in0=state[("pm", j)][:], scalar1=0.25, scalar2=None, op0=ALU.mult
            )

        def x_sums(i):
            px = ps_tp.tile([P, 8 * NX], F32, name="px", tag="tp")
            for bl in range(2):
                for ct in range(4):
                    for j in range(4):
                        nc.tensor.matmul(
                            out=px[:, NX * (4 * bl + ct) : NX * (4 * bl + ct + 1)],
                            lhsT=x_sb[2 * i + bl][:, C * j + P * ct : C * j + P * (ct + 1)],
                            rhs=ones[:],
                            start=(j == 0),
                            stop=(j == 3),
                        )
            nc.scalar.mul(
                out=xm4[:, 8 * i : 8 * (i + 1)].rearrange("p (c o) -> p c o", o=1),
                in_=px[:].rearrange("p (c n) -> p c n", n=NX)[:, :, 0:1],
                mul=1.0 / (4 * T),
            )

        def blend(b, ct, lo=0, hi=T):
            gt = state[("gt", b, ct)]
            nc.vector.scalar_tensor_tensor(
                out=gt[:, lo:hi], in0=memq[:, T * ct + lo : T * ct + hi],
                scalar=xm4[:, 4 * b + ct : 4 * b + ct + 1], in1=gt[:, lo:hi],
                op0=ALU.subtract, op1=ALU.mult,
            )

        def x_total():
            nc.vector.tensor_reduce(
                out=xbar[:], in_=xm4[:].rearrange("p (b c) -> p c b", c=4), axis=mybir.AxisListType.X, op=ALU.add
            )

        def add_last(b, ct):
            t0, t1 = state[("gt", 0, ct)], state[("gt", b, ct)]
            nc.vector.scalar_tensor_tensor(
                out=t0[:], in0=t1[:], scalar=xbar[:, ct : ct + 1], in1=t0[:], op0=ALU.add, op1=ALU.add
            )

        def add_up(b, ct):
            t0, t1 = state[("gt", 0, ct)], state[("gt", b, ct)]
            nc.vector.tensor_tensor(out=t0[:], in0=t0[:], in1=t1[:], op=ALU.add)

        def sum_part(b, half, ct):
            key = ("pf", half, ct // 2)
            if b == 0 and ct % 2 == 0:
                state[key] = ps_tp.tile([P, 512], F32, name="pf", tag="tp")
            pf = state[key]
            src = state[("gt", b, ct)]
            for tl in range(2):
                n = 2 * half + tl
                col = 256 * tl + P * (ct % 2)
                nc.tensor.matmul(
                    out=pf[:, col : col + P], lhsT=src[:, P * n : P * (n + 1)], rhs=ident32[:], is_transpose=True,
                    start=(b == 0 and ct % 2 == 0 and tl == 0), stop=(b == 3 and ct % 2 == 1 and tl == 1),
                )

        def store(half, pair, eng):
            ot = work.tile([P, 512], F32, name="ot", tag="ot", bufs=4)
            copy_on(eng, ot[:], state[("pf", half, pair)][:])
            nc.sync.dma_start(
                out=out[0].rearrange("(t p) c -> p t c", t=4)[:, 2 * half : 2 * half + 2, 256 * pair : 256 * (pair + 1)],
                in_=ot[:].rearrange("p (t c) -> p t c", t=2),
            )

        keep_clock(8)
        transposes(0, 0)
        evacs(0, 0, "SSSS")
        for g in range(4):
            quant_first(0, g)
        keep_clock(4)
        bias_transpose()
        regroup_w(0); quant_w(0)
        transposes(0, 1)
        evac(0, 1, 0, "S"); quant_first(1, 0); evac(0, 1, 1, "S"); quant_first(1, 1)
        evac(0, 1, 2, "S"); regroup_w(1); evac(0, 1, 3, "S")
        quant_first(1, 2); quant_w(1); quant_first(1, 3)
        first_passes(0)
        first_passes(1)
        split_words(1, 0, "S"); split_words(1, 1)
        regroup_w(2); quant_w(2); regroup_w(3)
        transposes(1, 0)
        evac(1, 0, 0, "S"); evac(1, 0, 1, "S"); quant_w(3)
        evac(1, 0, 2, "S"); evac(1, 0, 3, "S")
        split_words(1, 2); quant(1, 0, 0); split_words(1, 3)
        first_passes(2); first_passes(3); sigmoids(0)
        quant(1, 0, 1)
        memory_transposes(); memory_evac(0); memory_evac(1)
        transposes(1, 1); evacs(1, 1, "SSVV")
        x_sums(0)
        quant(1, 1, 0)
        all_passes(1, 0)
        quant(1, 1, 1); split_words(2, 0, "S"); split_words(2, 1); blend(0, 0); blend(0, 1)
        transposes(2, 0); evacs(2, 0, "SSSS")
        blend(0, 2); blend(0, 3); split_words(2, 2); quant(2, 0, 0); split_words(2, 3); quant(2, 0, 1)
        for ct in range(4):
            passes(1, 1, ct); sigmoid(1, ct)
        transposes(2, 1); evacs(2, 1, "SSSS")
        split_words(3, 0); blend(1, 0); split_words(3, 1); blend(1, 1); add_up(1, 0); quant(2, 1, 0); blend(1, 2); quant(2, 1, 1); blend(1, 3)
        all_passes(2, 0)
        split_words(3, 2, "S")
        x_sums(1)
        transposes(3, 0); evacs(3, 0, "SSSS")
        x_total(); add_up(1, 1); add_up(1, 2); quant(3, 0, 0); split_words(3, 3); quant(3, 0, 1)
        for ct in range(4):
            passes(2, 1, ct); sigmoid(2, ct)
        add_up(1, 3)
        transposes(3, 1); evacs(3, 1, "SSSS")
        blend(2, 0); blend(2, 1); add_last(2, 0); add_last(2, 1); quant(3, 1, 0); blend(2, 2); quant(3, 1, 1); blend(2, 3)
        all_passes(3, 0)
        for ct in range(4):
            sigmoid(3, ct, 0, 256)
        sum_part(0, 0, 0); sum_part(0, 0, 1); sum_part(0, 1, 0); sum_part(0, 1, 1)
        for ct in range(4):
            passes(3, 1, ct); sigmoid(3, ct, 256, 512)
        blend(3, 0, 0, 256); blend(3, 1, 0, 256)
        add_last(2, 2); add_last(2, 3)
        blend(3, 2, 0, 256); blend(3, 3, 0, 256)
        sum_part(3, 0, 0); sum_part(3, 0, 1); store(0, 0, "S")
        sum_part(0, 0, 2); sum_part(0, 0, 3)
        sum_part(0, 1, 2); sum_part(0, 1, 3)
        sum_part(3, 0, 2); sum_part(3, 0, 3); store(0, 1, "S")
        for ct in range(4):
            blend(3, ct, 256, 512)
        sum_part(3, 1, 0); sum_part(3, 1, 1); store(1, 0, "S")
        sum_part(3, 1, 2); sum_part(3, 1, 3); store(1, 1, "V")
